import numpy as np
import ml_dtypes


def mxq(x, axis, fmt="e4m3"):
    dtype, down = {"e4m3": (ml_dtypes.float8_e4m3fn, 7), "e5m2": (ml_dtypes.float8_e5m2, 14)}[fmt]
    v = np.moveaxis(np.asarray(x, np.float32).astype(ml_dtypes.bfloat16).astype(np.float64), axis, -1)
    blocks = v.reshape(v.shape[:-1] + (-1, 32))
    amax = np.abs(blocks).max(-1, keepdims=True)
    byte = np.maximum(np.where(amax > 0, np.frexp(amax)[1] - 1 + 127, 0) - down, 1)
    scale = np.exp2(byte - 127.0)
    codes = (blocks / scale).astype(np.float32).astype(dtype).astype(np.float64)
    return np.moveaxis((codes * scale).reshape(v.shape), -1, axis)


WIDE = False


def mx_kscale(k):
    if not WIDE:
        return np.ones(k)
    levels = np.array([18, -18])
    if k % 512:
        return np.exp2(np.random.permutation(np.resize(levels, k // 32))).repeat(32)
    a = np.empty((k // 512, 16))
    for p in range(k // 512):
        a[p, :8] = np.random.permutation(np.resize(levels, 8))
        for g in range(8):
            far = levels[np.abs(levels - a[p, g]) >= 10]
            a[p, g + 8] = far[np.random.randint(len(far))]
    return np.exp2(a.ravel()).repeat(32)


BF16 = ml_dtypes.bfloat16


def bf(x):
    return np.asarray(x, np.float32).astype(BF16)


def f64(x):
    return np.asarray(x).astype(np.float64)


B, C, T, H, W, AT, AF = 1, 1024, 8, 16, 16, 32, 48
D = C // 2
C2 = 2 * C
NKV = AT * AF
REP, REM = AT // T, AT % T
QS = np.sqrt(2.0 / np.sqrt(D))


def setup_inputs():
    st = mx_kscale(NKV)[::160][:T]
    sa = np.repeat(st, REP)
    s = np.repeat(sa, AF)
    up = mx_kscale(D)
    ug = mx_kscale(D)
    m = np.random.standard_normal((B, C, T))[..., None, None]
    v = bf((np.random.standard_normal((B, C, T, H, W)) + 0.7 * m) * st[None, None, :, None, None])
    a = bf(np.random.standard_normal((B, C, AT, AF)) * sa[None, None, :, None])
    Wp = bf(np.random.standard_normal((D, C2)) * 0.8 * QS / np.sqrt(C) / up[:, None])
    bp = bf(np.random.standard_normal(D) * 0.1)
    Wg = bf(np.random.standard_normal((D, C2)) / np.sqrt(C) / ug[:, None])
    bg = bf(np.random.standard_normal(D) * 0.1)
    g0 = bf(4.0 * np.random.standard_normal((B, D, NKV)) * np.exp2(np.random.randint(-6, 1, (B, 1, NKV))) / s[None, None, :] * up[None, :, None])
    g1 = bf(np.random.standard_normal((B, NKV, D)) * np.exp2(np.random.randint(-6, 1, (B, NKV, 1))) / s[None, :, None] * ug[None, None, :])
    return {"v": v, "a": a, "Wp": Wp, "bp": bp, "Wg": Wg, "bg": bg, "grad_0": g0, "grad_1": g1}


def joined(v, a):
    z = f64(v).mean(axis=(3, 4))
    z = np.repeat(z, REP, axis=2)
    z = np.broadcast_to(z[..., None], (B, C, AT, AF))
    return np.concatenate([f64(a), z], axis=1).reshape(B, C2, NKV)


def reference(v, a, Wp, bp, Wg, bg, grad_0, grad_1):
    av = joined(v, a)[0]
    dz = np.concatenate([f64(grad_0)[0], f64(grad_1)[0].T], axis=0)
    wa = np.concatenate([f64(Wp)[:, :C], f64(Wg)[:, :C]], axis=0)
    da = mxq(wa, 0, "e4m3").T @ mxq(dz, 0, "e5m2")
    dw = mxq(dz, 1, "e5m2") @ mxq(av, 1, "e4m3").T
    return da.reshape(B, C, AT, AF), dw[:D], dw[D:]

@@ -1,0 +1,417 @@
+from contextlib import ExitStack
+
+import concourse.mybir as mybir
+from concourse.masks import make_identity
+
+F32 = mybir.dt.float32
+BF16 = mybir.dt.bfloat16
+U32 = mybir.dt.uint32
+U8 = mybir.dt.uint8
+E4M3 = mybir.dt.float8_e4m3fn_x4
+E5M2 = mybir.dt.float8_e5m2_x4
+ADD = mybir.AluOpType.add
+MULT = mybir.AluOpType.mult
+AX = mybir.AxisListType.X
+
+P = 128
+C = 1024
+D = 512
+T = 8
+HW = 256
+NTOK = 1536
+G = 3
+FLOPS = 2 * (2 * D) * NTOK * C + 2 * (2 * D) * (2 * C) * NTOK
+BYTES = 2 * (C * T * HW + C * NTOK + 2 * D * C + 2 * D * NTOK) + 4 * (C * NTOK + 2 * D * 2 * C)
+
+
+def tile_nlgate_pa_v_kernel(tc, v, a, Wp, bp, Wg, bg, grad_0, grad_1, da, dWp, dWg):
+    nc = tc.nc
+    with ExitStack() as ctx:
+        const = ctx.enter_context(tc.tile_pool(name="const", bufs=1))
+        raw = ctx.enter_context(tc.tile_pool(name="raw", bufs=1))
+        work = ctx.enter_context(tc.tile_pool(name="work", bufs=1))
+        keep = ctx.enter_context(tc.tile_pool(name="keep", bufs=1))
+        psum = ctx.enter_context(tc.psum_pool(name="psum", bufs=1))
+
+        identf = const.tile([P, P], F32, name="identf")
+        identb = const.tile([P, P], BF16, name="identb")
+        make_identity(nc, identf[:])
+        make_identity(nc, identb[:])
+
+        v_hbm = v[0].rearrange("(n c) t h w -> n c (t h w)", c=P)
+        a_hbm = a[0].rearrange("(n c) i f -> n c (i f)", c=P)
+        g0_hbm = grad_0[0].rearrange("(p j) k -> p j k", j=4)
+        g1_hbm = grad_1[0].rearrange("(b g r t) w -> r b g (t w)", b=16, g=G, r=8, t=4)
+        vt = {}
+        at = {}
+        wt = {}
+        g0 = raw.tile([P, 4, NTOK], BF16, name="g0", align_bytes=64)
+        g1 = raw.tile([P, G, 2048], BF16, name="g1", align_bytes=64)
+
+        def load_v(n):
+            vt[n] = raw.tile([P, 2048], BF16, name="r4", tag="r4", bufs=12, align_bytes=64)
+            nc.sync.dma_start(out=vt[n][:], in_=v_hbm[n])
+
+        def load_a(n):
+            at[n] = raw.tile([P, 2048], BF16, name="r4", tag="r4", bufs=12, align_bytes=64)
+            nc.sync.dma_start(out=at[n][:, 0:NTOK], in_=a_hbm[n])
+
+        def load_w(l):
+            wt[l] = raw.tile([P, 4, C], BF16, name="w", tag="w", bufs=2, align_bytes=64)
+            src = (Wp, Wg)[l].rearrange("(p j) c -> p j c", j=4)
+            nc.sync.dma_start(out=wt[l][:], in_=src[:, :, 0:C])
+
+        def load_g0(h):
+            nc.sync.dma_start(out=g0[:, 2 * h : 2 * h + 2, :], in_=g0_hbm[:, 2 * h : 2 * h + 2, :])
+
+        def operand(name):
+            codes = keep.tile([P, 512], U32, name=name + "c", tag=name + "c", align_bytes=64)
+            scales = keep.tile([P, 512], U8, name=name + "s", tag=name + "s", align_bytes=64)
+            return codes, scales
+
+        def new_qin():
+            return work.tile([P, 2048], BF16, name="qin", tag="qin", bufs=9, align_bytes=64)
+
+        def quantize(name, src, fmt):
+            op = operand(name)
+            nc.vector.quantize_mx(out=op[0][:].bitcast(fmt), scales=op[1][:], in_=src)
+            return op
+
+        def bank():
+            return psum.tile([P, 512], F32, name="tp", tag="tp", bufs=3)
+
+        def presort(src, engine):
+            s = work.tile([P, 768], F32, name="srt", tag="srt", bufs=5, align_bytes=64)
+            i = src.bitcast(F32).rearrange("p (b g r u) -> p u b g r", b=16, g=G, r=8, u=2)
+            o = s[:].rearrange("p (g u b r) -> p u b g r", b=16, g=G, r=8, u=2)
+            for u in range(2):
+                copy(engine, o[:, u], i[:, u])
+            return s
+
+        def copy(engine, out, in_):
+            if engine == "S":
+                nc.scalar.copy(out, in_)
+            else:
+                nc.vector.tensor_copy(out=out, in_=in_)
+
+        def interleave(engine, src):
+            q = new_qin()
+            copy(engine, q[:].rearrange("p (c j) -> p c j", j=4), src.rearrange("p j c -> p c j"))
+            return q
+
+        def weave(main, fill):
+            done = 0
+            for i, step in enumerate(main):
+                step()
+                while done < len(fill) and done < (i + 1) * len(fill) / len(main):
+                    fill[done]()
+                    done += 1
+
+        g1F = work.tile([P, NTOK * 4], BF16, name="g1F", align_bytes=64)
+        g1F_words = g1F[:].bitcast(F32).rearrange("p (b x) -> p b x", b=16)
+        dT0 = {}
+        dT1 = {}
+        dF0 = {}
+        dF1 = {}
+        wa = {}
+        zz = {}
+        q1 = {}
+        q0 = {}
+
+        def g1_transposes(g, t0, engine):
+            words = g1[:, g, :].bitcast(F32)
+            b = bank()
+            for k in range(4):
+                t, u = t0 + k // 2, k % 2
+                nc.tensor.transpose(b[:, k * P : (k + 1) * P], words[:, t * 256 + u : (t + 1) * 256 : 2], identf[:])
+            dst = g1F_words[:, :, 64 * g : 64 * g + 64].rearrange("p b (r y) -> p b r y", r=8)
+            copy(engine, dst[:, :, :, 2 * t0 : 2 * t0 + 4], b[:].rearrange("p (k b r) -> p b r k", k=4, r=8))
+
+        def g1_interleave(g, engine):
+            q1[g] = interleave(engine, g1[:, g, :].rearrange("p (t f) -> p t f", t=4))
+
+        def g1_quantize(g):
+            dT1[g] = quantize("dT1%d" % g, q1[g][:], E5M2)
+
+        def g1F_quantize(n):
+            dF1[n] = quantize("dF1%d" % n, g1F[:, n * 2048 : (n + 1) * 2048], E5M2)
+
+        zbank = {}
+        zrep = {}
+        zq = {}
+
+        def v_sum(n):
+            h, i = n // 4, n % 4
+            if i == 0:
+                zbank[h] = psum.tile([P, 512], F32, name="zb", tag="zb", bufs=1)
+            view = vt[n][:].rearrange("p (t s w) -> p s t w", t=T, s=16)
+            o = zbank[h][:, i * P : (i + 1) * P].rearrange("p (t w) -> p t w", t=T)
+            for s in range(16):
+                nc.tensor.matmul(o, identb[:], view[:, s], start=(s == 0), stop=(s == 15))
+
+        def z_mean(h):
+            zs = work.tile([P, 32], F32, name="zs", tag="zs", bufs=2)
+            nc.vector.tensor_reduce(out=zs[:], in_=zbank[h][:].rearrange("p (x w) -> p x w", w=16), op=ADD, axis=AX)
+            zrep[h] = work.tile([P, 512], BF16, name="zr", tag="zr", bufs=2)
+            nc.vector.tensor_scalar(
+                out=zrep[h][:].rearrange("p (x w) -> p x w", w=16),
+                in0=zs[:].unsqueeze(2).to_broadcast([P, 32, 16]),
+                scalar1=1.0 / HW,
+                scalar2=None,
+                op0=MULT,
+            )
+
+        def z_transpose(h, engine):
+            zt = psum.tile([P, 512], BF16, name="tp", tag="tp", bufs=3)
+            for i in range(4):
+                nc.tensor.transpose(zt[:, i * P : (i + 1) * P], zrep[h][:, i * P : (i + 1) * P], identb[:])
+            zq[h] = new_qin()
+            dst = zq[h][:].rearrange("p (c t) -> p c t", t=4)
+            for i in range(2):
+                c = slice(256 * i, 256 * (i + 1))
+                copy(engine[i], dst[:, c], zt[:, c].unsqueeze(2).to_broadcast([P, 256, 4]))
+
+        def z_quantize(h):
+            zz[h] = [quantize("zz%d" % h, zq[h][:], E4M3)] * G
+
+        dWp_rows = dWp.rearrange("(p j) c -> j p c", j=4)
+        dWg_rows = dWg.rearrange("(n p) c -> n p c", p=P)
+        da_rows = da[0].rearrange("(n p) i f -> n p (i f)", p=P)
+
+        def matmuls(pairs, m, dst, engine):
+            acc = psum.tile([P, 512], F32, name="acc", tag="acc", bufs=4)
+            cols = slice(m * P, (m + 1) * P)
+            for k, ((lc, ls), lf, (rc, rs), rf) in enumerate(pairs):
+                nc.tensor.matmul_mx(
+                    out=acc[:],
+                    lhsT=lc[:, cols].bitcast(lf),
+                    lhsT_scale=ls[:, cols],
+                    rhs=rc[:].bitcast(rf),
+                    rhs_scale=rs[:],
+                    start=(k == 0),
+                    stop=(k == len(pairs) - 1),
+                )
+            o = work.tile([P, 512], F32, name="ost", tag="ost", bufs=10)
+            copy(engine, o[:], acc[:])
+            nc.sync.dma_start(out=dst, in_=o[:])
+
+        def token_product(dT, rows, right, h, m, col0, engine):
+            pairs = [(dT[g], E5M2, right[h][g], E4M3) for g in range(G)]
+            matmuls(pairs, m, rows[m][:, col0 + h * 512 : col0 + h * 512 + 512], engine)
+
+        def audio_product(ct, n, engine):
+            h = ct // 4
+            pairs = [(wa[h], E4M3, dF0[n], E5M2), (wa[2 + h], E4M3, dF1[n], E5M2)]
+            matmuls(pairs, ct % 4, da_rows[ct][:, n * 512 : (n + 1) * 512], engine)
+
+        s0 = {}
+
+        def g0_presort(j, engine):
+            s0[j] = presort(g0[:, j, :], engine)
+
+        def g0_transposes(g, j0, engine):
+            if j0 == 0:
+                q0[g] = new_qin()
+            b = bank()
+            for k in range(4):
+                j, u = j0 + k // 2, k % 2
+                nc.tensor.transpose(b[:, k * P : (k + 1) * P], s0[j][:, (2 * g + u) * P : (2 * g + u + 1) * P], identf[:])
+            copy(
+                engine,
+                q0[g][:].bitcast(F32)[:, j0 * 256 : j0 * 256 + 512].rearrange("p (j c u) -> p j c u", j=2, u=2),
+                b[:].rearrange("p (j u c) -> p j c u", j=2, u=2),
+            )
+
+        def g0_quantize(g):
+            dT0[g] = quantize("dT0%d" % g, q0[g][:], E5M2)
+
+        qf = {}
+
+        def g0F_interleave(n, engine):
+            qf[n] = interleave(engine, g0[:, :, n * 512 : (n + 1) * 512])
+
+        def g0F_quantize(n):
+            dF0[n] = quantize("dF0%d" % n, qf[n][:], E5M2)
+
+        qw = {}
+
+        def wa_interleave(l, h, engine):
+            qw[l, h] = interleave(engine, wt[l][:, :, h * 512 : (h + 1) * 512])
+
+        def wa_quantize(l, h):
+            wa[2 * l + h] = quantize("wa%d" % (2 * l + h), qw[l, h][:], E4M3)
+
+        sa = {}
+        qa = {}
+        ac = {0: {}, 1: {}}
+
+        def a_presort(n, engine):
+            sa[n] = presort(at[n][:, 0:NTOK], engine)
+
+        def a_transposes(h, i0, g, engine):
+            if i0 == 0:
+                qa[h, g] = new_qin()
+            b = bank()
+            for k in range(4):
+                n, u = 4 * h + i0 + k // 2, k % 2
+                nc.tensor.transpose(b[:, k * P : (k + 1) * P], sa[n][:, (2 * g + u) * P : (2 * g + u + 1) * P], identf[:])
+            copy(
+                engine,
+                qa[h, g][:].bitcast(F32)[:, i0 * 256 : i0 * 256 + 512].rearrange("p (j c u) -> p j c u", j=2, u=2),
+                b[:].rearrange("p (j u c) -> p j c u", j=2, u=2),
+            )
+
+        def a_quantize(h, g):
+            ac[h][g] = quantize("a%d%d" % (h, g), qa[h, g][:], E4M3)
+
+        with tc.manual_schedule():
+            for r in range(8):
+                nc.sync.dma_start(out=g1[r:P:8], in_=g1_hbm[r])
+            for n in range(4):
+                load_v(n)
+            load_g0(0)
+            load_g0(1)
+            for n in (4, 5, 6, 7):
+                load_v(n)
+            load_w(0)
+            load_w(1)
+            for n in range(8):
+                load_a(n)
+            g1_interleave(2, "V")
+            g1_transposes(1, 0, "S")
+            g1_transposes(1, 2, "V")
+            g1_transposes(0, 0, "S")
+            g1_interleave(1, "S")
+            v_sum(0)
+            g1_transposes(0, 2, "S")
+            g1_transposes(2, 2, "S")
+            g1_interleave(0, "V")
+            g1_quantize(1)
+            v_sum(1)
+            v_sum(3)
+            g0_presort(0, "S")
+            g0_presort(1, "V")
+            v_sum(2)
+            g1_quantize(0)
+            g1_quantize(2)
+            g1_transposes(2, 0, "S")
+            g0_transposes(1, 0, "S")
+            z_mean(0)
+            g0_presort(2, "V")
+            g0_transposes(0, 0, "V")
+            g0_presort(3, "S")
+            g0_transposes(2, 0, "S")
+            v_sum(4)
+            g1F_quantize(2)
+            g0_transposes(1, 2, "V")
+            g0F_interleave(0, "V")
+            g0_transposes(0, 2, "V")
+            z_transpose(0, "SSV")
+            g0_quantize(1)
+            z_quantize(0)
+            v_sum(5)
+            g1F_quantize(0)
+            g0_transposes(2, 2, "S")
+            v_sum(6)
+            wa_interleave(0, 0, "S")
+            v_sum(7)
+            z_mean(1)
+            g0_quantize(2)
+            g0_quantize(0)
+            token_product(dT1, dWg_rows, zz, 0, 3, C, "S")
+            g0F_quantize(0)
+            token_product(dT1, dWg_rows, zz, 0, 1, C, "V")
+            token_product(dT1, dWg_rows, zz, 0, 0, C, "S")
+            z_transpose(1, "SSV")
+            token_product(dT1, dWg_rows, zz, 0, 2, C, "S")
+            token_product(dT0, dWp_rows, zz, 0, 1, C, "S")
+            g1F_quantize(1)
+            wa_quantize(0, 0)
+            token_product(dT0, dWp_rows, zz, 0, 0, C, "S")
+            token_product(dT0, dWp_rows, zz, 0, 3, C, "S")
+            a_presort(0, "V")
+            a_presort(1, "V")
+            a_presort(2, "S")
+            z_quantize(1)
+            a_presort(4, "V")
+            a_presort(3, "V")
+            a_transposes(0, 0, 0, "S")
+            a_transposes(0, 0, 1, "V")
+            a_transposes(0, 0, 2, "S")
+            token_product(dT1, dWg_rows, zz, 1, 0, C, "S")
+            wa_interleave(1, 0, "V")
+            token_product(dT1, dWg_rows, zz, 1, 3, C, "V")
+            token_product(dT0, dWp_rows, zz, 1, 0, C, "S")
+            token_product(dT0, dWp_rows, zz, 0, 2, C, "V")
+            a_transposes(0, 2, 2, "S")
+            a_transposes(0, 2, 0, "S")
+            a_presort(5, "S")
+            a_transposes(0, 2, 1, "V")
+            a_quantize(0, 1)
+            token_product(dT0, dWp_rows, zz, 1, 1, C, "S")
+            token_product(dT0, dWp_rows, zz, 1, 2, C, "S")
+            a_quantize(0, 0)
+            a_quantize(0, 2)
+            token_product(dT0, dWp_rows, zz, 1, 3, C, "V")
+            wa_interleave(0, 1, "S")
+            wa_interleave(1, 1, "V")
+            token_product(dT0, dWp_rows, ac, 0, 3, 0, "V")
+            token_product(dT1, dWg_rows, zz, 1, 2, C, "S")
+            token_product(dT0, dWp_rows, ac, 0, 1, 0, "S")
+            a_presort(6, "V")
+            token_product(dT0, dWp_rows, ac, 0, 0, 0, "S")
+            wa_quantize(1, 0)
+            a_presort(7, "V")
+            token_product(dT1, dWg_rows, zz, 1, 1, C, "S")
+            wa_quantize(1, 1)
+            a_transposes(1, 0, 1, "S")
+            g0F_interleave(2, "V")
+            a_transposes(1, 0, 0, "S")
+            g0F_interleave(1, "V")
+            a_transposes(1, 0, 2, "S")
+            wa_quantize(0, 1)
+            g0F_quantize(1)
+            token_product(dT1, dWg_rows, ac, 0, 0, 0, "S")
+            token_product(dT1, dWg_rows, ac, 0, 2, 0, "V")
+            g0F_quantize(2)
+            audio_product(1, 0, "S")
+            audio_product(3, 0, "V")
+            a_transposes(1, 2, 0, "S")
+            a_transposes(1, 2, 2, "V")
+            a_transposes(1, 2, 1, "V")
+            a_quantize(1, 0)
+            audio_product(5, 0, "S")
+            token_product(dT1, dWg_rows, ac, 0, 3, 0, "S")
+            audio_product(0, 2, "S")
+            a_quantize(1, 2)
+            audio_product(6, 2, "S")
+            audio_product(2, 2, "V")
+            audio_product(1, 1, "S")
+            audio_product(7, 1, "V")
+            audio_product(7, 0, "V")
+            audio_product(4, 2, "V")
+            audio_product(4, 1, "V")
+            audio_product(5, 2, "V")
+            token_product(dT0, dWp_rows, ac, 0, 2, 0, "S")
+            a_quantize(1, 1)
+            audio_product(6, 1, "S")
+            audio_product(2, 1, "V")
+            token_product(dT0, dWp_rows, ac, 1, 0, 0, "S")
+            token_product(dT0, dWp_rows, ac, 1, 3, 0, "S")
+            audio_product(4, 0, "S")
+            audio_product(1, 2, "V")
+            token_product(dT1, dWg_rows, ac, 1, 0, 0, "V")
+            audio_product(0, 1, "V")
+            token_product(dT0, dWp_rows, ac, 1, 2, 0, "S")
+            audio_product(2, 0, "V")
+            audio_product(6, 0, "S")
+            token_product(dT1, dWg_rows, ac, 1, 3, 0, "V")
+            audio_product(5, 1, "V")
+            token_product(dT0, dWp_rows, ac, 1, 1, 0, "S")
+            audio_product(7, 2, "V")
+            audio_product(3, 1, "S")
+            token_product(dT1, dWg_rows, ac, 1, 1, 0, "S")
+            audio_product(3, 2, "S")
+            audio_product(0, 0, "S")
+            token_product(dT1, dWg_rows, ac, 0, 1, 0, "V")
+            token_product(dT1, dWg_rows, ac, 1, 2, 0, "S")

@@ -38,8 +38,8 @@ def tile_nlgate_pa_v_kernel(tc, v, a, Wp, bp, Wg, bg, grad_0, grad_1, da, dWp, d
         make_identity(nc, identf[:])
         make_identity(nc, identb[:])
 
-        v_hbm = v[0].rearrange("(n c) t h w -> n c (t h w)", c=P)
-        a_hbm = a[0].rearrange("(n c) i f -> n c (i f)", c=P)
+        v_hbm = v[0].rearrange("(n p i) t h w -> n p i (t h w)", p=P, i=2)
+        a_hbm = a[0].rearrange("(n p i) x f -> n p i (x f)", p=P, i=2)
         g0_hbm = grad_0[0].rearrange("(p j) k -> p j k", j=4)
         g1_hbm = grad_1[0].rearrange("(b g r t) w -> r b g (t w)", b=16, g=G, r=8, t=4)
         vt = {}
@@ -48,21 +48,27 @@ def tile_nlgate_pa_v_kernel(tc, v, a, Wp, bp, Wg, bg, grad_0, grad_1, da, dWp, d
         g0 = raw.tile([P, 4, NTOK], BF16, name="g0", align_bytes=64)
         g1 = raw.tile([P, G, 2048], BF16, name="g1", align_bytes=64)
 
+        def raw_tile():
+            return raw.tile([P, 4096], BF16, name="r8", tag="r8", bufs=7, align_bytes=64)
+
         def load_v(n):
-            vt[n] = raw.tile([P, 2048], BF16, name="r4", tag="r4", bufs=12, align_bytes=64)
-            nc.sync.dma_start(out=vt[n][:], in_=v_hbm[n])
+            vt[n] = raw_tile()[:].rearrange("p (i x) -> p i x", i=2)
+            nc.sync.dma_start(out=vt[n], in_=v_hbm[n])
 
         def load_a(n):
-            at[n] = raw.tile([P, 2048], BF16, name="r4", tag="r4", bufs=12, align_bytes=64)
-            nc.sync.dma_start(out=at[n][:, 0:NTOK], in_=a_hbm[n])
+            at[n] = raw_tile()[:, 0 : 2 * NTOK].rearrange("p (i x) -> p i x", i=2)
+            nc.sync.dma_start(out=at[n], in_=a_hbm[n])
 
         def load_w(l):
-            wt[l] = raw.tile([P, 4, C], BF16, name="w", tag="w", bufs=2, align_bytes=64)
+            wt[l] = raw_tile()[:].rearrange("p (j c) -> p j c", j=4)
             src = (Wp, Wg)[l].rearrange("(p j) c -> p j c", j=4)
-            nc.sync.dma_start(out=wt[l][:], in_=src[:, :, 0:C])
+            nc.sync.dma_start(out=wt[l], in_=src[:, :, 0:C])
 
         def load_g0(h):
             nc.sync.dma_start(out=g0[:, 2 * h : 2 * h + 2, :], in_=g0_hbm[:, 2 * h : 2 * h + 2, :])
+
+        def load_g1(r):
+            nc.scalar.dma_start(out=g1[r:P:8], in_=g1_hbm[r])
 
         def operand(name):
             codes = keep.tile([P, 512], U32, name=name + "c", tag=name + "c", align_bytes=64)
@@ -70,7 +76,7 @@ def tile_nlgate_pa_v_kernel(tc, v, a, Wp, bp, Wg, bg, grad_0, grad_1, da, dWp, d
             return codes, scales
 
         def new_qin():
-            return work.tile([P, 2048], BF16, name="qin", tag="qin", bufs=9, align_bytes=64)
+            return work.tile([P, 2048], BF16, name="qin", tag="qin", bufs=8, align_bytes=64)
 
         def quantize(name, src, fmt):
             op = operand(name)
@@ -78,7 +84,7 @@ def tile_nlgate_pa_v_kernel(tc, v, a, Wp, bp, Wg, bg, grad_0, grad_1, da, dWp, d
             return op
 
         def bank():
-            return psum.tile([P, 512], F32, name="tp", tag="tp", bufs=3)
+            return psum.tile([P, 512], F32, name="tp", tag="tp", bufs=4)
 
         def presort(src, engine):
             s = work.tile([P, 768], F32, name="srt", tag="srt", bufs=5, align_bytes=64)
@@ -136,40 +142,43 @@ def tile_nlgate_pa_v_kernel(tc, v, a, Wp, bp, Wg, bg, grad_0, grad_1, da, dWp, d
         def g1F_quantize(n):
             dF1[n] = quantize("dF1%d" % n, g1F[:, n * 2048 : (n + 1) * 2048], E5M2)
 
-        zbank = {}
+        zsum = {}
         zrep = {}
         zq = {}
 
-        def v_sum(n):
-            h, i = n // 4, n % 4
-            if i == 0:
-                zbank[h] = psum.tile([P, 512], F32, name="zb", tag="zb", bufs=1)
-            view = vt[n][:].rearrange("p (t s w) -> p s t w", t=T, s=16)
-            o = zbank[h][:, i * P : (i + 1) * P].rearrange("p (t w) -> p t w", t=T)
-            for s in range(16):
-                nc.tensor.matmul(o, identb[:], view[:, s], start=(s == 0), stop=(s == 15))
+        def v_sum(n, engine):
+            h, i = n // 2, n % 2
+            if h not in zsum:
+                zsum[h] = work.tile([P, 32], F32, name="zs", tag="zs", bufs=2)
+            b = bank()
+            for k in range(2):
+                view = vt[n][:, k, :].rearrange("p (t s w) -> p s t w", t=T, s=8)
+                o = b[:, k * 256 : (k + 1) * 256].rearrange("p (t w) -> p t w", t=T)
+                for s in range(8):
+                    nc.tensor.matmul(o, identb[:], view[:, s], start=(s == 0), stop=(s == 7))
+            nc.vector.tensor_reduce(
+                out=zsum[h][:, 16 * i : 16 * i + 16], in_=b[:].rearrange("p (x w) -> p x w", w=32), op=ADD, axis=AX
+            )
 
         def z_mean(h):
-            zs = work.tile([P, 32], F32, name="zs", tag="zs", bufs=2)
-            nc.vector.tensor_reduce(out=zs[:], in_=zbank[h][:].rearrange("p (x w) -> p x w", w=16), op=ADD, axis=AX)
             zrep[h] = work.tile([P, 512], BF16, name="zr", tag="zr", bufs=2)
             nc.vector.tensor_scalar(
                 out=zrep[h][:].rearrange("p (x w) -> p x w", w=16),
-                in0=zs[:].unsqueeze(2).to_broadcast([P, 32, 16]),
+                in0=zsum[h][:].unsqueeze(2).to_broadcast([P, 32, 16]),
                 scalar1=1.0 / HW,
                 scalar2=None,
                 op0=MULT,
             )
 
         def z_transpose(h, engine):
-            zt = psum.tile([P, 512], BF16, name="tp", tag="tp", bufs=3)
+            zt = psum.tile([P, 512], BF16, name="tp", tag="tp", bufs=4)
             for i in range(4):
                 nc.tensor.transpose(zt[:, i * P : (i + 1) * P], zrep[h][:, i * P : (i + 1) * P], identb[:])
             zq[h] = new_qin()
-            dst = zq[h][:].rearrange("p (c t) -> p c t", t=4)
-            for i in range(2):
-                c = slice(256 * i, 256 * (i + 1))
-                copy(engine[i], dst[:, c], zt[:, c].unsqueeze(2).to_broadcast([P, 256, 4]))
+            for n in range(2):
+                dst = zq[h][:, n * 1024 : (n + 1) * 1024].rearrange("q (p i t) -> q p i t", i=2, t=4)
+                src = zt[:, n * 256 : (n + 1) * 256].rearrange("q (i p) -> q p i", i=2)
+                copy(engine[n], dst, src.unsqueeze(3).to_broadcast([P, P, 2, 4]))
 
         def z_quantize(h):
             zz[h] = [quantize("zz%d" % h, zq[h][:], E4M3)] * G
@@ -178,7 +187,7 @@ def tile_nlgate_pa_v_kernel(tc, v, a, Wp, bp, Wg, bg, grad_0, grad_1, da, dWp, d
         dWg_rows = dWg.rearrange("(n p) c -> n p c", p=P)
         da_rows = da[0].rearrange("(n p) i f -> n p (i f)", p=P)
 
-        def matmuls(pairs, m, dst, engine):
+        def matmuls(pairs, m, o, engine):
             acc = psum.tile([P, 512], F32, name="acc", tag="acc", bufs=4)
             cols = slice(m * P, (m + 1) * P)
             for k, ((lc, ls), lf, (rc, rs), rf) in enumerate(pairs):
@@ -191,18 +200,25 @@ def tile_nlgate_pa_v_kernel(tc, v, a, Wp, bp, Wg, bg, grad_0, grad_1, da, dWp, d
                     start=(k == 0),
                     stop=(k == len(pairs) - 1),
                 )
-            o = work.tile([P, 512], F32, name="ost", tag="ost", bufs=10)
-            copy(engine, o[:], acc[:])
-            nc.sync.dma_start(out=dst, in_=o[:])
+            copy(engine, o, acc[:])
 
-        def token_product(dT, rows, right, h, m, col0, engine):
-            pairs = [(dT[g], E5M2, right[h][g], E4M3) for g in range(G)]
-            matmuls(pairs, m, rows[m][:, col0 + h * 512 : col0 + h * 512 + 512], engine)
+        def out_tile():
+            return work.tile([P, NTOK], F32, name="ost", tag="ost", bufs=5)
 
-        def audio_product(ct, n, engine):
+        def token_product(dT, rows, right, m, col0, engines):
+            o = out_tile()
+            for h in range(2):
+                pairs = [(dT[g], E5M2, right[h][g], E4M3) for g in range(G)]
+                matmuls(pairs, m, o[:, h * 512 : (h + 1) * 512], engines[h])
+            nc.sync.dma_start(out=rows[m][:, col0 : col0 + C], in_=o[:, 0:C])
+
+        def audio_product(ct, engines):
             h = ct // 4
-            pairs = [(wa[h], E4M3, dF0[n], E5M2), (wa[2 + h], E4M3, dF1[n], E5M2)]
-            matmuls(pairs, ct % 4, da_rows[ct][:, n * 512 : (n + 1) * 512], engine)
+            o = out_tile()
+            for n in range(G):
+                pairs = [(wa[h], E4M3, dF0[n], E5M2), (wa[2 + h], E4M3, dF1[n], E5M2)]
+                matmuls(pairs, ct % 4, o[:, n * 512 : (n + 1) * 512], engines[n])
+            nc.sync.dma_start(out=da_rows[ct], in_=o[:])
 
         s0 = {}
 
@@ -210,7 +226,7 @@ def tile_nlgate_pa_v_kernel(tc, v, a, Wp, bp, Wg, bg, grad_0, grad_1, da, dWp, d
             s0[j] = presort(g0[:, j, :], engine)
 
         def g0_transposes(g, j0, engine):
-            if j0 == 0:
+            if g not in q0:
                 q0[g] = new_qin()
             b = bank()
             for k in range(4):
@@ -245,173 +261,143 @@ def tile_nlgate_pa_v_kernel(tc, v, a, Wp, bp, Wg, bg, grad_0, grad_1, da, dWp, d
         qa = {}
         ac = {0: {}, 1: {}}
 
-        def a_presort(n, engine):
-            sa[n] = presort(at[n][:, 0:NTOK], engine)
+        def a_presort(n, i, engine):
+            sa[n, i] = presort(at[n][:, i, :], engine)
 
-        def a_transposes(h, i0, g, engine):
-            if i0 == 0:
+        def a_transposes(n, g, engine):
+            h = n // 2
+            if (h, g) not in qa:
                 qa[h, g] = new_qin()
             b = bank()
             for k in range(4):
-                n, u = 4 * h + i0 + k // 2, k % 2
-                nc.tensor.transpose(b[:, k * P : (k + 1) * P], sa[n][:, (2 * g + u) * P : (2 * g + u + 1) * P], identf[:])
-            copy(
-                engine,
-                qa[h, g][:].bitcast(F32)[:, i0 * 256 : i0 * 256 + 512].rearrange("p (j c u) -> p j c u", j=2, u=2),
-                b[:].rearrange("p (j u c) -> p j c u", j=2, u=2),
-            )
+                i, u = k // 2, k % 2
+                nc.tensor.transpose(b[:, k * P : (k + 1) * P], sa[n, i][:, (2 * g + u) * P : (2 * g + u + 1) * P], identf[:])
+            words = qa[h, g][:].bitcast(F32)[:, (n % 2) * 512 : (n % 2) * 512 + 512]
+            copy(engine, words.rearrange("q (c k) -> q c k", k=4), b[:].rearrange("q (k c) -> q c k", k=4))
 
         def a_quantize(h, g):
             ac[h][g] = quantize("a%d%d" % (h, g), qa[h, g][:], E4M3)
 
         with tc.manual_schedule():
-            for r in range(8):
-                nc.sync.dma_start(out=g1[r:P:8], in_=g1_hbm[r])
-            for n in range(4):
-                load_v(n)
+            load_v(0)
+            load_g1(0)
+            load_g1(4)
+            load_g1(1)
+            load_g1(5)
+            load_v(1)
+            load_g1(2)
+            load_g1(6)
+            load_g1(3)
+            load_g1(7)
+            load_v(2)
+            load_v(3)
             load_g0(0)
             load_g0(1)
-            for n in (4, 5, 6, 7):
-                load_v(n)
             load_w(0)
+            load_a(0)
+            load_a(1)
             load_w(1)
-            for n in range(8):
-                load_a(n)
-            g1_interleave(2, "V")
-            g1_transposes(1, 0, "S")
+            load_a(2)
+            load_a(3)
+            v_sum(0, "V")
+            g1_interleave(2, "S")
+            g1_interleave(1, "V")
+            v_sum(1, "V")
             g1_transposes(1, 2, "V")
-            g1_transposes(0, 0, "S")
-            g1_interleave(1, "S")
-            v_sum(0)
-            g1_transposes(0, 2, "S")
             g1_transposes(2, 2, "S")
-            g1_interleave(0, "V")
-            g1_quantize(1)
-            v_sum(1)
-            v_sum(3)
-            g0_presort(0, "S")
-            g0_presort(1, "V")
-            v_sum(2)
-            g1_quantize(0)
-            g1_quantize(2)
-            g1_transposes(2, 0, "S")
-            g0_transposes(1, 0, "S")
             z_mean(0)
-            g0_presort(2, "V")
-            g0_transposes(0, 0, "V")
-            g0_presort(3, "S")
-            g0_transposes(2, 0, "S")
-            v_sum(4)
-            g1F_quantize(2)
-            g0_transposes(1, 2, "V")
-            g0F_interleave(0, "V")
-            g0_transposes(0, 2, "V")
-            z_transpose(0, "SSV")
-            g0_quantize(1)
+            g1_transposes(1, 0, "V")
+            g1_transposes(0, 0, "S")
+            g1_quantize(1)
+            g1_quantize(2)
+            g1_interleave(0, "V")
+            g1_transposes(0, 2, "V")
+            z_transpose(0, "SS")
+            v_sum(2, "V")
             z_quantize(0)
-            v_sum(5)
-            g1F_quantize(0)
-            g0_transposes(2, 2, "S")
-            v_sum(6)
-            wa_interleave(0, 0, "S")
-            v_sum(7)
+            g0_presort(1, "S")
+            g1_quantize(0)
+            g0_presort(0, "S")
+            g0_presort(3, "S")
+            v_sum(3, "V")
+            g0_transposes(1, 0, "S")
+            g0_transposes(2, 0, "V")
             z_mean(1)
-            g0_quantize(2)
-            g0_quantize(0)
-            token_product(dT1, dWg_rows, zz, 0, 3, C, "S")
-            g0F_quantize(0)
-            token_product(dT1, dWg_rows, zz, 0, 1, C, "V")
-            token_product(dT1, dWg_rows, zz, 0, 0, C, "S")
-            z_transpose(1, "SSV")
-            token_product(dT1, dWg_rows, zz, 0, 2, C, "S")
-            token_product(dT0, dWp_rows, zz, 0, 1, C, "S")
-            g1F_quantize(1)
-            wa_quantize(0, 0)
-            token_product(dT0, dWp_rows, zz, 0, 0, C, "S")
-            token_product(dT0, dWp_rows, zz, 0, 3, C, "S")
-            a_presort(0, "V")
-            a_presort(1, "V")
-            a_presort(2, "S")
+            g0_transposes(0, 0, "S")
+            g1_transposes(2, 0, "S")
+            g0_presort(2, "V")
+            z_transpose(1, "VS")
             z_quantize(1)
-            a_presort(4, "V")
-            a_presort(3, "V")
-            a_transposes(0, 0, 0, "S")
-            a_transposes(0, 0, 1, "V")
-            a_transposes(0, 0, 2, "S")
-            token_product(dT1, dWg_rows, zz, 1, 0, C, "S")
-            wa_interleave(1, 0, "V")
-            token_product(dT1, dWg_rows, zz, 1, 3, C, "V")
-            token_product(dT0, dWp_rows, zz, 1, 0, C, "S")
-            token_product(dT0, dWp_rows, zz, 0, 2, C, "V")
-            a_transposes(0, 2, 2, "S")
-            a_transposes(0, 2, 0, "S")
-            a_presort(5, "S")
-            a_transposes(0, 2, 1, "V")
-            a_quantize(0, 1)
-            token_product(dT0, dWp_rows, zz, 1, 1, C, "S")
-            token_product(dT0, dWp_rows, zz, 1, 2, C, "S")
+            g0_transposes(0, 2, "S")
+            a_presort(0, 0, "V")
+            g0_transposes(1, 2, "S")
+            g0_transposes(2, 2, "S")
+            g0_quantize(0)
+            a_presort(0, 1, "V")
+            token_product(dT1, dWg_rows, zz, 3, C, "VV")
+            a_presort(1, 0, "V")
+            a_presort(1, 1, "S")
+            g1F_quantize(0)
+            g0F_interleave(2, "S")
+            token_product(dT1, dWg_rows, zz, 2, C, "SV")
+            g0_quantize(1)
+            a_presort(2, 1, "V")
+            g0_quantize(2)
+            token_product(dT1, dWg_rows, zz, 0, C, "SV")
+            a_transposes(0, 1, "S")
+            g0F_quantize(2)
+            a_transposes(0, 0, "S")
+            a_transposes(1, 0, "S")
+            a_transposes(0, 2, "S")
+            a_presort(3, 1, "S")
+            a_presort(3, 0, "S")
+            wa_interleave(0, 1, "V")
+            token_product(dT0, dWp_rows, zz, 3, C, "VS")
+            token_product(dT0, dWp_rows, zz, 2, C, "SV")
             a_quantize(0, 0)
+            a_transposes(1, 2, "V")
+            a_transposes(1, 1, "V")
+            a_presort(2, 0, "S")
+            a_transposes(3, 2, "S")
             a_quantize(0, 2)
-            token_product(dT0, dWp_rows, zz, 1, 3, C, "V")
-            wa_interleave(0, 1, "S")
+            a_transposes(3, 0, "S")
+            g0F_interleave(0, "V")
+            token_product(dT1, dWg_rows, zz, 1, C, "SS")
+            token_product(dT0, dWp_rows, zz, 0, C, "SS")
+            a_quantize(0, 1)
+            a_transposes(2, 0, "S")
+            wa_interleave(1, 0, "V")
+            a_transposes(3, 1, "S")
+            a_transposes(2, 1, "S")
+            a_transposes(2, 2, "V")
+            a_quantize(1, 0)
+            token_product(dT0, dWp_rows, zz, 1, C, "SS")
+            a_quantize(1, 1)
+            a_quantize(1, 2)
+            token_product(dT1, dWg_rows, ac, 0, 0, "SS")
             wa_interleave(1, 1, "V")
-            token_product(dT0, dWp_rows, ac, 0, 3, 0, "V")
-            token_product(dT1, dWg_rows, zz, 1, 2, C, "S")
-            token_product(dT0, dWp_rows, ac, 0, 1, 0, "S")
-            a_presort(6, "V")
-            token_product(dT0, dWp_rows, ac, 0, 0, 0, "S")
-            wa_quantize(1, 0)
-            a_presort(7, "V")
-            token_product(dT1, dWg_rows, zz, 1, 1, C, "S")
-            wa_quantize(1, 1)
-            a_transposes(1, 0, 1, "S")
-            g0F_interleave(2, "V")
-            a_transposes(1, 0, 0, "S")
+            g1F_quantize(1)
+            token_product(dT0, dWp_rows, ac, 0, 0, "SS")
             g0F_interleave(1, "V")
-            a_transposes(1, 0, 2, "S")
+            token_product(dT1, dWg_rows, ac, 1, 0, "SS")
+            g1F_quantize(2)
             wa_quantize(0, 1)
             g0F_quantize(1)
-            token_product(dT1, dWg_rows, ac, 0, 0, 0, "S")
-            token_product(dT1, dWg_rows, ac, 0, 2, 0, "V")
-            g0F_quantize(2)
-            audio_product(1, 0, "S")
-            audio_product(3, 0, "V")
-            a_transposes(1, 2, 0, "S")
-            a_transposes(1, 2, 2, "V")
-            a_transposes(1, 2, 1, "V")
-            a_quantize(1, 0)
-            audio_product(5, 0, "S")
-            token_product(dT1, dWg_rows, ac, 0, 3, 0, "S")
-            audio_product(0, 2, "S")
-            a_quantize(1, 2)
-            audio_product(6, 2, "S")
-            audio_product(2, 2, "V")
-            audio_product(1, 1, "S")
-            audio_product(7, 1, "V")
-            audio_product(7, 0, "V")
-            audio_product(4, 2, "V")
-            audio_product(4, 1, "V")
-            audio_product(5, 2, "V")
-            token_product(dT0, dWp_rows, ac, 0, 2, 0, "S")
-            a_quantize(1, 1)
-            audio_product(6, 1, "S")
-            audio_product(2, 1, "V")
-            token_product(dT0, dWp_rows, ac, 1, 0, 0, "S")
-            token_product(dT0, dWp_rows, ac, 1, 3, 0, "S")
-            audio_product(4, 0, "S")
-            audio_product(1, 2, "V")
-            token_product(dT1, dWg_rows, ac, 1, 0, 0, "V")
-            audio_product(0, 1, "V")
-            token_product(dT0, dWp_rows, ac, 1, 2, 0, "S")
-            audio_product(2, 0, "V")
-            audio_product(6, 0, "S")
-            token_product(dT1, dWg_rows, ac, 1, 3, 0, "V")
-            audio_product(5, 1, "V")
-            token_product(dT0, dWp_rows, ac, 1, 1, 0, "S")
-            audio_product(7, 2, "V")
-            audio_product(3, 1, "S")
-            token_product(dT1, dWg_rows, ac, 1, 1, 0, "S")
-            audio_product(3, 2, "S")
-            audio_product(0, 0, "S")
-            token_product(dT1, dWg_rows, ac, 0, 1, 0, "V")
-            token_product(dT1, dWg_rows, ac, 1, 2, 0, "S")
+            wa_quantize(1, 0)
+            g0F_quantize(0)
+            token_product(dT1, dWg_rows, ac, 2, 0, "SS")
+            wa_quantize(1, 1)
+            wa_interleave(0, 0, "S")
+            token_product(dT0, dWp_rows, ac, 2, 0, "VV")
+            audio_product(6, "VSV")
+            wa_quantize(0, 0)
+            audio_product(7, "VSS")
+            audio_product(1, "VVV")
+            token_product(dT0, dWp_rows, ac, 3, 0, "VV")
+            audio_product(5, "SVS")
+            audio_product(4, "VSS")
+            audio_product(2, "VVS")
+            audio_product(3, "VSV")
+            audio_product(0, "VVS")
+            token_product(dT0, dWp_rows, ac, 1, 0, "SV")
+            token_product(dT1, dWg_rows, ac, 3, 0, "VS")

@@ -41,7 +41,7 @@ def tile_nlgate_pa_v_kernel(tc, v, a, Wp, bp, Wg, bg, grad_0, grad_1, da, dWp, d
         v_hbm = v[0].rearrange("(n p i) t h w -> n p i (t h w)", p=P, i=2)
         a_hbm = a[0].rearrange("(n p i) x f -> n p i (x f)", p=P, i=2)
         g0_hbm = grad_0[0].rearrange("(p j) k -> p j k", j=4)
-        g1_hbm = grad_1[0].rearrange("(b g r t) w -> r b g (t w)", b=16, g=G, r=8, t=4)
+        g1_hbm = grad_1[0].rearrange("(b g r t) w -> g b r (t w)", b=16, g=G, r=8, t=4)
         vt = {}
         at = {}
         wt = {}
@@ -49,11 +49,12 @@ def tile_nlgate_pa_v_kernel(tc, v, a, Wp, bp, Wg, bg, grad_0, grad_1, da, dWp, d
         g1 = raw.tile([P, G, 2048], BF16, name="g1", align_bytes=64)
 
         def raw_tile():
-            return raw.tile([P, 4096], BF16, name="r8", tag="r8", bufs=7, align_bytes=64)
+            return raw.tile([P, 4096], BF16, name="r8", tag="r8", bufs=6, align_bytes=64)
 
-        def load_v(n):
-            vt[n] = raw_tile()[:].rearrange("p (i x) -> p i x", i=2)
-            nc.sync.dma_start(out=vt[n], in_=v_hbm[n])
+        def load_v(n, k):
+            if n not in vt:
+                vt[n] = raw_tile()[:].rearrange("p (i x) -> p i x", i=2)
+            nc.sync.dma_start(out=vt[n][:, k, :], in_=v_hbm[n][:, k, :])
 
         def load_a(n):
             at[n] = raw_tile()[:, 0 : 2 * NTOK].rearrange("p (i x) -> p i x", i=2)
@@ -65,10 +66,10 @@ def tile_nlgate_pa_v_kernel(tc, v, a, Wp, bp, Wg, bg, grad_0, grad_1, da, dWp, d
             nc.sync.dma_start(out=wt[l], in_=src[:, :, 0:C])
 
         def load_g0(h):
-            nc.sync.dma_start(out=g0[:, 2 * h : 2 * h + 2, :], in_=g0_hbm[:, 2 * h : 2 * h + 2, :])
+            nc.sync.dma_start(out=g0[:, h : h + 1, :], in_=g0_hbm[:, h : h + 1, :])
 
-        def load_g1(r):
-            nc.scalar.dma_start(out=g1[r:P:8], in_=g1_hbm[r])
+        def load_g1(g, cols=slice(0, 2048)):
+            nc.sync.dma_start(out=g1[:, g, cols], in_=g1_hbm[g][:, :, cols])
 
         def operand(name):
             codes = keep.tile([P, 512], U32, name=name + "c", tag=name + "c", align_bytes=64)
@@ -102,7 +103,8 @@ def tile_nlgate_pa_v_kernel(tc, v, a, Wp, bp, Wg, bg, grad_0, grad_1, da, dWp, d
 
         def interleave(engine, src):
             q = new_qin()
-            copy(engine, q[:].rearrange("p (c j) -> p c j", j=4), src.rearrange("p j c -> p c j"))
+            dst = q[:].rearrange("p (c i j) -> p c j i", i=4, j=4)
+            copy(engine, dst, src.rearrange("p j (c i) -> p c j i", i=4))
             return q
 
         def weave(main, fill):
@@ -124,12 +126,18 @@ def tile_nlgate_pa_v_kernel(tc, v, a, Wp, bp, Wg, bg, grad_0, grad_1, da, dWp, d
         q1 = {}
         q0 = {}
 
-        def g1_transposes(g, t0, engine):
+        banks = {}
+
+        def g1_transpose(g, t0):
             words = g1[:, g, :].bitcast(F32)
             b = bank()
             for k in range(4):
                 t, u = t0 + k // 2, k % 2
                 nc.tensor.transpose(b[:, k * P : (k + 1) * P], words[:, t * 256 + u : (t + 1) * 256 : 2], identf[:])
+            banks["g1", g, t0] = b
+
+        def g1_unload(g, t0, engine):
+            b = banks["g1", g, t0]
             dst = g1F_words[:, :, 64 * g : 64 * g + 64].rearrange("p b (r y) -> p b r y", r=8)
             copy(engine, dst[:, :, :, 2 * t0 : 2 * t0 + 4], b[:].rearrange("p (k b r) -> p b r k", k=4, r=8))
 
@@ -146,19 +154,48 @@ def tile_nlgate_pa_v_kernel(tc, v, a, Wp, bp, Wg, bg, grad_0, grad_1, da, dWp, d
         zrep = {}
         zq = {}
 
-        def v_sum(n, engine):
+        def v_matmul(n, k):
+            if ("v", n) not in banks:
+                banks["v", n] = bank()
+            view = vt[n][:, k, :].rearrange("p (t s w) -> p s t w", t=T, s=8)
+            o = banks["v", n][:, k * 256 : (k + 1) * 256].rearrange("p (t w) -> p t w", t=T)
+            for s in range(8):
+                nc.tensor.matmul(o, identb[:], view[:, s], start=(s == 0), stop=(s == 7))
+
+        def v_reduce(n):
             h, i = n // 2, n % 2
-            if h not in zsum:
-                zsum[h] = work.tile([P, 32], F32, name="zs", tag="zs", bufs=2)
-            b = bank()
-            for k in range(2):
-                view = vt[n][:, k, :].rearrange("p (t s w) -> p s t w", t=T, s=8)
-                o = b[:, k * 256 : (k + 1) * 256].rearrange("p (t w) -> p t w", t=T)
-                for s in range(8):
-                    nc.tensor.matmul(o, identb[:], view[:, s], start=(s == 0), stop=(s == 7))
+            new_zsum(h)
+            b = banks["v", n]
             nc.vector.tensor_reduce(
                 out=zsum[h][:, 16 * i : 16 * i + 16], in_=b[:].rearrange("p (x w) -> p x w", w=32), op=ADD, axis=AX
             )
+
+        def new_zsum(h):
+            if h not in zsum:
+                zsum[h] = work.tile([P, 32], F32, name="zs", tag="zs", bufs=2)
+
+        def v_sum_v(n, k):
+            h, i = n // 2, n % 2
+            new_zsum(h)
+            nc.vector.tensor_reduce(
+                out=zsum[h][:, 16 * i + 8 * k : 16 * i + 8 * k + 8],
+                in_=vt[n][:, k, :].rearrange("p (t x) -> p t x", t=T),
+                op=ADD,
+                axis=AX,
+            )
+
+        def v_sum_s(n, k, t0):
+            h, i = n // 2, n % 2
+            new_zsum(h)
+            for t in range(t0, t0 + 2):
+                junk = work.tile([P, HW], BF16, name="junk", tag="junk", bufs=2)
+                c = 16 * i + 8 * k + t
+                nc.scalar.activation(
+                    out=junk[:],
+                    in_=vt[n][:, k, t * HW : (t + 1) * HW],
+                    func=mybir.ActivationFunctionType.Copy,
+                    accum_out=zsum[h][:, c : c + 1],
+                )
 
         def z_mean(h):
             zrep[h] = work.tile([P, 512], BF16, name="zr", tag="zr", bufs=2)
@@ -170,15 +207,18 @@ def tile_nlgate_pa_v_kernel(tc, v, a, Wp, bp, Wg, bg, grad_0, grad_1, da, dWp, d
                 op0=MULT,
             )
 
-        def z_transpose(h, engine):
+        def z_transpose(h):
             zt = psum.tile([P, 512], BF16, name="tp", tag="tp", bufs=4)
             for i in range(4):
                 nc.tensor.transpose(zt[:, i * P : (i + 1) * P], zrep[h][:, i * P : (i + 1) * P], identb[:])
-            zq[h] = new_qin()
-            for n in range(2):
-                dst = zq[h][:, n * 1024 : (n + 1) * 1024].rearrange("q (p i t) -> q p i t", i=2, t=4)
-                src = zt[:, n * 256 : (n + 1) * 256].rearrange("q (i p) -> q p i", i=2)
-                copy(engine[n], dst, src.unsqueeze(3).to_broadcast([P, P, 2, 4]))
+            banks["z", h] = zt
+
+        def z_spread(h, n, engine):
+            if h not in zq:
+                zq[h] = new_qin()
+            dst = zq[h][:, n * 1024 : (n + 1) * 1024].rearrange("q (p i t) -> q p i t", i=2, t=4)
+            src = banks["z", h][:, n * 256 : (n + 1) * 256].rearrange("q (i p) -> q p i", i=2)
+            copy(engine, dst, src.unsqueeze(3).to_broadcast([P, P, 2, 4]))
 
         def z_quantize(h):
             zz[h] = [quantize("zz%d" % h, zq[h][:], E4M3)] * G
@@ -187,7 +227,9 @@ def tile_nlgate_pa_v_kernel(tc, v, a, Wp, bp, Wg, bg, grad_0, grad_1, da, dWp, d
         dWg_rows = dWg.rearrange("(n p) c -> n p c", p=P)
         da_rows = da[0].rearrange("(n p) i f -> n p (i f)", p=P)
 
-        def matmuls(pairs, m, o, engine):
+        outs = {}
+
+        def matmuls(pairs, m):
             acc = psum.tile([P, 512], F32, name="acc", tag="acc", bufs=4)
             cols = slice(m * P, (m + 1) * P)
             for k, ((lc, ls), lf, (rc, rs), rf) in enumerate(pairs):
@@ -200,42 +242,54 @@ def tile_nlgate_pa_v_kernel(tc, v, a, Wp, bp, Wg, bg, grad_0, grad_1, da, dWp, d
                     start=(k == 0),
                     stop=(k == len(pairs) - 1),
                 )
-            copy(engine, o, acc[:])
+            return acc
 
-        def out_tile():
-            return work.tile([P, NTOK], F32, name="ost", tag="ost", bufs=5)
+        def token_unload(l, z, m, h, engine):
+            outs[l, z, m, h] = work.tile([P, 512], F32, name="tok", tag="tok", bufs=10)
+            copy(engine, outs[l, z, m, h][:], banks[l, z, m, h][:])
 
-        def token_product(dT, rows, right, m, col0, engines):
-            o = out_tile()
-            for h in range(2):
-                pairs = [(dT[g], E5M2, right[h][g], E4M3) for g in range(G)]
-                matmuls(pairs, m, o[:, h * 512 : (h + 1) * 512], engines[h])
-            nc.sync.dma_start(out=rows[m][:, col0 : col0 + C], in_=o[:, 0:C])
+        def token_store(l, z, m, h):
+            rows = (dWp_rows, dWg_rows)[l]
+            c = z * C + h * 512
+            nc.sync.dma_start(out=rows[m][:, c : c + 512], in_=outs[l, z, m, h][:])
 
-        def audio_product(ct, engines):
+        def audio_unload(ct, n, engine):
+            if ct not in outs:
+                outs[ct] = work.tile([P, NTOK], F32, name="aud", tag="aud", bufs=3)
+            copy(engine, outs[ct][:, n * 512 : (n + 1) * 512], banks["da", ct, n][:])
+
+        def token_matmul(l, z, m, h):
+            dT = (dT0, dT1)[l]
+            right = (ac, zz)[z]
+            banks[l, z, m, h] = matmuls([(dT[g], E5M2, right[h][g], E4M3) for g in range(G)], m)
+
+        def audio_matmul(ct, n):
             h = ct // 4
-            o = out_tile()
-            for n in range(G):
-                pairs = [(wa[h], E4M3, dF0[n], E5M2), (wa[2 + h], E4M3, dF1[n], E5M2)]
-                matmuls(pairs, ct % 4, o[:, n * 512 : (n + 1) * 512], engines[n])
-            nc.sync.dma_start(out=da_rows[ct], in_=o[:])
+            pairs = [(wa[h], E4M3, dF0[n], E5M2), (wa[2 + h], E4M3, dF1[n], E5M2)]
+            banks["da", ct, n] = matmuls(pairs, ct % 4)
+
+        def audio_store(ct):
+            nc.sync.dma_start(out=da_rows[ct], in_=outs[ct][:])
 
         s0 = {}
 
         def g0_presort(j, engine):
             s0[j] = presort(g0[:, j, :], engine)
 
-        def g0_transposes(g, j0, engine):
-            if g not in q0:
-                q0[g] = new_qin()
+        def g0_transpose(g, j0):
             b = bank()
             for k in range(4):
                 j, u = j0 + k // 2, k % 2
                 nc.tensor.transpose(b[:, k * P : (k + 1) * P], s0[j][:, (2 * g + u) * P : (2 * g + u + 1) * P], identf[:])
+            banks["g0", g, j0] = b
+
+        def g0_unload(g, j0, engine):
+            if g not in q0:
+                q0[g] = new_qin()
             copy(
                 engine,
                 q0[g][:].bitcast(F32)[:, j0 * 256 : j0 * 256 + 512].rearrange("p (j c u) -> p j c u", j=2, u=2),
-                b[:].rearrange("p (j u c) -> p j c u", j=2, u=2),
+                banks["g0", g, j0][:].rearrange("p (j u c) -> p j c u", j=2, u=2),
             )
 
         def g0_quantize(g):
@@ -264,140 +318,314 @@ def tile_nlgate_pa_v_kernel(tc, v, a, Wp, bp, Wg, bg, grad_0, grad_1, da, dWp, d
         def a_presort(n, i, engine):
             sa[n, i] = presort(at[n][:, i, :], engine)
 
-        def a_transposes(n, g, engine):
-            h = n // 2
-            if (h, g) not in qa:
-                qa[h, g] = new_qin()
+        def a_transpose(n, g):
             b = bank()
             for k in range(4):
                 i, u = k // 2, k % 2
                 nc.tensor.transpose(b[:, k * P : (k + 1) * P], sa[n, i][:, (2 * g + u) * P : (2 * g + u + 1) * P], identf[:])
+            banks["a", n, g] = b
+
+        def a_unload(n, g, engine):
+            h = n // 2
+            if (h, g) not in qa:
+                qa[h, g] = new_qin()
             words = qa[h, g][:].bitcast(F32)[:, (n % 2) * 512 : (n % 2) * 512 + 512]
-            copy(engine, words.rearrange("q (c k) -> q c k", k=4), b[:].rearrange("q (k c) -> q c k", k=4))
+            copy(engine, words.rearrange("q (c k) -> q c k", k=4), banks["a", n, g][:].rearrange("q (k c) -> q c k", k=4))
 
         def a_quantize(h, g):
             ac[h][g] = quantize("a%d%d" % (h, g), qa[h, g][:], E4M3)
 
         with tc.manual_schedule():
-            load_v(0)
-            load_g1(0)
-            load_g1(4)
+            load_g1(0, slice(0, 1024))
+            load_g1(0, slice(1024, 2048))
             load_g1(1)
-            load_g1(5)
-            load_v(1)
             load_g1(2)
-            load_g1(6)
-            load_g1(3)
-            load_g1(7)
-            load_v(2)
-            load_v(3)
+            load_v(0, 0)
+            load_v(0, 1)
+            load_v(1, 0)
+            load_v(1, 1)
             load_g0(0)
             load_g0(1)
+            load_g0(2)
+            load_g0(3)
+            load_v(2, 0)
+            load_v(2, 1)
+            load_v(3, 0)
+            load_v(3, 1)
             load_w(0)
+            load_w(1)
             load_a(0)
             load_a(1)
-            load_w(1)
             load_a(2)
             load_a(3)
-            v_sum(0, "V")
-            g1_interleave(2, "S")
-            g1_interleave(1, "V")
-            v_sum(1, "V")
-            g1_transposes(1, 2, "V")
-            g1_transposes(2, 2, "S")
-            z_mean(0)
-            g1_transposes(1, 0, "V")
-            g1_transposes(0, 0, "S")
-            g1_quantize(1)
-            g1_quantize(2)
+            g1_transpose(0, 0)
             g1_interleave(0, "V")
-            g1_transposes(0, 2, "V")
-            z_transpose(0, "SS")
-            v_sum(2, "V")
-            z_quantize(0)
-            g0_presort(1, "S")
+            g1_transpose(0, 2)
+            g1_unload(0, 0, "S")
+            g1_interleave(1, "S")
+            g1_transpose(1, 2)
+            g1_unload(0, 2, "V")
+            g1_transpose(1, 0)
             g1_quantize(0)
-            g0_presort(0, "S")
-            g0_presort(3, "S")
-            v_sum(3, "V")
-            g0_transposes(1, 0, "S")
-            g0_transposes(2, 0, "V")
-            z_mean(1)
-            g0_transposes(0, 0, "S")
-            g1_transposes(2, 0, "S")
-            g0_presort(2, "V")
-            z_transpose(1, "VS")
-            z_quantize(1)
-            g0_transposes(0, 2, "S")
-            a_presort(0, 0, "V")
-            g0_transposes(1, 2, "S")
-            g0_transposes(2, 2, "S")
-            g0_quantize(0)
-            a_presort(0, 1, "V")
-            token_product(dT1, dWg_rows, zz, 3, C, "VV")
-            a_presort(1, 0, "V")
-            a_presort(1, 1, "S")
-            g1F_quantize(0)
-            g0F_interleave(2, "S")
-            token_product(dT1, dWg_rows, zz, 2, C, "SV")
-            g0_quantize(1)
-            a_presort(2, 1, "V")
-            g0_quantize(2)
-            token_product(dT1, dWg_rows, zz, 0, C, "SV")
-            a_transposes(0, 1, "S")
-            g0F_quantize(2)
-            a_transposes(0, 0, "S")
-            a_transposes(1, 0, "S")
-            a_transposes(0, 2, "S")
-            a_presort(3, 1, "S")
-            a_presort(3, 0, "S")
-            wa_interleave(0, 1, "V")
-            token_product(dT0, dWp_rows, zz, 3, C, "VS")
-            token_product(dT0, dWp_rows, zz, 2, C, "SV")
-            a_quantize(0, 0)
-            a_transposes(1, 2, "V")
-            a_transposes(1, 1, "V")
-            a_presort(2, 0, "S")
-            a_transposes(3, 2, "S")
-            a_quantize(0, 2)
-            a_transposes(3, 0, "S")
-            g0F_interleave(0, "V")
-            token_product(dT1, dWg_rows, zz, 1, C, "SS")
-            token_product(dT0, dWp_rows, zz, 0, C, "SS")
-            a_quantize(0, 1)
-            a_transposes(2, 0, "S")
-            wa_interleave(1, 0, "V")
-            a_transposes(3, 1, "S")
-            a_transposes(2, 1, "S")
-            a_transposes(2, 2, "V")
-            a_quantize(1, 0)
-            token_product(dT0, dWp_rows, zz, 1, C, "SS")
-            a_quantize(1, 1)
-            a_quantize(1, 2)
-            token_product(dT1, dWg_rows, ac, 0, 0, "SS")
-            wa_interleave(1, 1, "V")
-            g1F_quantize(1)
-            token_product(dT0, dWp_rows, ac, 0, 0, "SS")
-            g0F_interleave(1, "V")
-            token_product(dT1, dWg_rows, ac, 1, 0, "SS")
+            g1_transpose(2, 2)
+            g1_unload(1, 2, "V")
+            g1_transpose(2, 0)
+            g1_unload(1, 0, "V")
+            v_matmul(0, 0)
+            g1_unload(2, 2, "V")
+            g1_interleave(2, "S")
+            g1_quantize(1)
+            v_matmul(0, 1)
+            g1_unload(2, 0, "V")
             g1F_quantize(2)
-            wa_quantize(0, 1)
-            g0F_quantize(1)
-            wa_quantize(1, 0)
-            g0F_quantize(0)
-            token_product(dT1, dWg_rows, ac, 2, 0, "SS")
-            wa_quantize(1, 1)
+            v_matmul(1, 0)
+            g1F_quantize(0)
+            g1_quantize(2)
+            v_matmul(1, 1)
+            v_reduce(0)
+            g0_presort(0, "S")
+            g1F_quantize(1)
+            g0_presort(1, "V")
+            v_reduce(1)
+            g0_transpose(0, 0)
+            g0_transpose(1, 0)
+            g0_presort(2, "V")
+            g0_unload(0, 0, "S")
+            g0_transpose(2, 0)
+            z_mean(0)
+            g0_unload(1, 0, "S")
+            g0_presort(3, "V")
+            z_transpose(0)
+            g0F_interleave(1, "V")
+            g0_unload(2, 0, "S")
+            g0_transpose(2, 2)
+            g0_transpose(0, 2)
+            z_spread(0, 0, "S")
+            v_matmul(2, 0)
+            z_spread(0, 1, "V")
+            g0_unload(0, 2, "S")
+            v_matmul(2, 1)
+            g0F_interleave(2, "S")
+            g0_unload(2, 2, "V")
+            z_quantize(0)
+            g0_transpose(1, 2)
+            g0_quantize(2)
+            token_matmul(1, 1, 1, 0)
+            v_reduce(2)
+            g0_unload(1, 2, "S")
+            g0_quantize(0)
+            token_matmul(1, 1, 3, 0)
+            v_sum_s(3, 0, 0)
+            g0F_quantize(2)
+            token_matmul(1, 1, 2, 0)
+            token_unload(1, 1, 1, 0, "S")
+            g0_quantize(1)
             wa_interleave(0, 0, "S")
-            token_product(dT0, dWp_rows, ac, 2, 0, "VV")
-            audio_product(6, "VSV")
+            token_unload(1, 1, 3, 0, "V")
+            token_store(1, 1, 1, 0)
+            token_matmul(0, 1, 1, 0)
+            token_unload(1, 1, 2, 0, "V")
+            token_store(1, 1, 3, 0)
+            token_matmul(0, 1, 3, 0)
+            g0F_quantize(1)
+            token_store(1, 1, 2, 0)
+            token_unload(0, 1, 1, 0, "V")
+            token_matmul(0, 1, 0, 0)
+            wa_interleave(1, 0, "V")
+            token_unload(0, 1, 3, 0, "S")
+            token_store(0, 1, 1, 0)
+            v_sum_s(3, 1, 0)
+            token_matmul(0, 1, 2, 0)
+            token_store(0, 1, 3, 0)
+            a_presort(0, 0, "S")
+            a_presort(0, 1, "V")
+            token_matmul(1, 1, 0, 0)
+            token_unload(0, 1, 0, 0, "V")
+            token_unload(0, 1, 2, 0, "S")
             wa_quantize(0, 0)
-            audio_product(7, "VSS")
-            audio_product(1, "VVV")
-            token_product(dT0, dWp_rows, ac, 3, 0, "VV")
-            audio_product(5, "SVS")
-            audio_product(4, "VSS")
-            audio_product(2, "VVS")
-            audio_product(3, "VSV")
-            audio_product(0, "VVS")
-            token_product(dT0, dWp_rows, ac, 1, 0, "SV")
-            token_product(dT1, dWg_rows, ac, 3, 0, "VS")
+            token_store(0, 1, 0, 0)
+            a_transpose(0, 0)
+            v_sum_s(3, 0, 2)
+            wa_quantize(1, 0)
+            token_store(0, 1, 2, 0)
+            a_transpose(0, 2)
+            a_unload(0, 0, "S")
+            a_transpose(0, 1)
+            token_unload(1, 1, 0, 0, "V")
+            audio_matmul(2, 2)
+            a_unload(0, 2, "S")
+            a_presort(1, 0, "V")
+            a_unload(0, 1, "S")
+            audio_matmul(3, 1)
+            g0F_interleave(0, "V")
+            token_store(1, 1, 0, 0)
+            a_presort(1, 1, "S")
+            audio_matmul(1, 1)
+            audio_matmul(3, 2)
+            v_sum_s(3, 0, 6)
+            audio_unload(3, 1, "V")
+            a_transpose(1, 1)
+            a_presort(3, 0, "S")
+            a_presort(3, 1, "V")
+            a_transpose(1, 2)
+            audio_unload(2, 2, "V")
+            a_transpose(1, 0)
+            audio_unload(1, 1, "S")
+            a_transpose(3, 0)
+            g0F_quantize(0)
+            a_unload(1, 0, "S")
+            audio_matmul(2, 1)
+            a_unload(3, 0, "V")
+            a_presort(2, 0, "S")
+            audio_matmul(3, 0)
+            audio_unload(3, 2, "V")
+            audio_matmul(1, 0)
+            audio_unload(2, 1, "V")
+            a_unload(1, 2, "S")
+            audio_unload(3, 0, "V")
+            v_sum_s(3, 1, 4)
+            audio_matmul(2, 0)
+            a_quantize(0, 2)
+            a_presort(2, 1, "S")
+            audio_matmul(1, 2)
+            audio_store(3)
+            a_unload(1, 1, "V")
+            audio_matmul(0, 2)
+            audio_unload(2, 0, "S")
+            audio_unload(1, 2, "V")
+            a_transpose(2, 2)
+            v_sum_s(3, 1, 6)
+            audio_store(2)
+            a_quantize(0, 1)
+            a_transpose(2, 0)
+            a_unload(2, 2, "S")
+            a_transpose(2, 1)
+            audio_unload(1, 0, "V")
+            a_transpose(3, 1)
+            wa_interleave(1, 1, "S")
+            a_transpose(3, 2)
+            a_unload(2, 1, "V")
+            audio_store(1)
+            audio_matmul(0, 0)
+            a_quantize(0, 0)
+            audio_matmul(0, 1)
+            audio_unload(0, 2, "V")
+            token_matmul(0, 0, 0, 0)
+            audio_unload(0, 0, "V")
+            a_unload(3, 2, "S")
+            audio_unload(0, 1, "V")
+            token_matmul(0, 0, 1, 0)
+            a_unload(3, 1, "S")
+            wa_quantize(1, 1)
+            audio_store(0)
+            token_unload(0, 0, 0, 0, "S")
+            a_quantize(1, 2)
+            token_matmul(0, 0, 2, 0)
+            token_unload(0, 0, 1, 0, "S")
+            a_quantize(1, 1)
+            token_store(0, 0, 0, 0)
+            wa_interleave(0, 1, "S")
+            token_matmul(1, 0, 2, 0)
+            token_store(0, 0, 1, 0)
+            a_unload(2, 0, "V")
+            token_unload(0, 0, 2, 0, "V")
+            token_matmul(1, 0, 0, 0)
+            a_quantize(1, 0)
+            token_store(0, 0, 2, 0)
+            token_matmul(1, 0, 1, 0)
+            token_unload(1, 0, 0, 0, "V")
+            token_unload(1, 0, 2, 0, "S")
+            wa_quantize(0, 1)
+            token_matmul(1, 0, 2, 1)
+            token_store(1, 0, 0, 0)
+            token_unload(1, 0, 1, 0, "S")
+            token_store(1, 0, 2, 0)
+            v_sum_s(3, 0, 4)
+            audio_matmul(6, 2)
+            token_store(1, 0, 1, 0)
+            token_unload(1, 0, 2, 1, "V")
+            v_sum_s(3, 1, 2)
+            audio_matmul(7, 1)
+            audio_unload(6, 2, "V")
+            token_store(1, 0, 2, 1)
+            audio_matmul(7, 2)
+            z_mean(1)
+            audio_unload(7, 1, "V")
+            audio_matmul(6, 0)
+            audio_unload(7, 2, "V")
+            audio_matmul(6, 1)
+            audio_unload(6, 0, "S")
+            token_matmul(1, 0, 1, 1)
+            audio_unload(6, 1, "S")
+            audio_matmul(4, 1)
+            audio_store(6)
+            token_unload(1, 0, 1, 1, "S")
+            token_matmul(1, 0, 0, 1)
+            audio_unload(4, 1, "S")
+            token_store(1, 0, 1, 1)
+            audio_matmul(4, 0)
+            token_unload(1, 0, 0, 1, "V")
+            audio_matmul(4, 2)
+            audio_unload(4, 0, "S")
+            token_store(1, 0, 0, 1)
+            audio_matmul(5, 2)
+            audio_unload(4, 2, "V")
+            token_matmul(0, 0, 2, 1)
+            audio_store(4)
+            audio_unload(5, 2, "S")
+            token_matmul(0, 0, 3, 0)
+            token_unload(0, 0, 2, 1, "S")
+            token_matmul(1, 0, 3, 1)
+            token_store(0, 0, 2, 1)
+            token_unload(0, 0, 3, 0, "V")
+            token_matmul(0, 0, 1, 1)
+            token_store(0, 0, 3, 0)
+            token_unload(1, 0, 3, 1, "V")
+            audio_matmul(5, 1)
+            token_store(1, 0, 3, 1)
+            token_unload(0, 0, 1, 1, "S")
+            z_transpose(1)
+            audio_unload(5, 1, "S")
+            token_store(0, 0, 1, 1)
+            token_matmul(0, 0, 0, 1)
+            z_spread(1, 0, "V")
+            token_matmul(0, 0, 3, 1)
+            token_unload(0, 0, 0, 1, "S")
+            z_spread(1, 1, "V")
+            token_matmul(1, 0, 3, 0)
+            token_store(0, 0, 0, 1)
+            token_unload(0, 0, 3, 1, "V")
+            audio_matmul(5, 0)
+            z_quantize(1)
+            token_store(0, 0, 3, 1)
+            token_unload(1, 0, 3, 0, "S")
+            audio_matmul(7, 0)
+            audio_unload(5, 0, "V")
+            token_store(1, 0, 3, 0)
+            token_matmul(1, 1, 0, 1)
+            audio_unload(7, 0, "V")
+            audio_store(5)
+            token_matmul(0, 1, 1, 1)
+            audio_store(7)
+            token_unload(1, 1, 0, 1, "S")
+            token_matmul(0, 1, 3, 1)
+            token_store(1, 1, 0, 1)
+            token_unload(0, 1, 1, 1, "S")
+            token_matmul(1, 1, 2, 1)
+            token_store(0, 1, 1, 1)
+            token_unload(0, 1, 3, 1, "V")
+            token_matmul(0, 1, 0, 1)
+            token_store(0, 1, 3, 1)
+            token_unload(1, 1, 2, 1, "S")
+            token_matmul(1, 1, 3, 1)
+            token_store(1, 1, 2, 1)
+            token_unload(0, 1, 0, 1, "S")
+            token_matmul(0, 1, 2, 1)
+            token_store(0, 1, 0, 1)
+            token_unload(1, 1, 3, 1, "S")
+            token_matmul(1, 1, 1, 1)
+            token_store(1, 1, 3, 1)
+            token_unload(0, 1, 2, 1, "S")
+            token_store(0, 1, 2, 1)
+            token_unload(1, 1, 1, 1, "S")
+            token_store(1, 1, 1, 1)

from contextlib import ExitStack

import concourse.mybir as mybir
from concourse.masks import make_identity

F32 = mybir.dt.float32
BF16 = mybir.dt.bfloat16
U32 = mybir.dt.uint32
U8 = mybir.dt.uint8
E4M3 = mybir.dt.float8_e4m3fn_x4
E5M2 = mybir.dt.float8_e5m2_x4
ADD = mybir.AluOpType.add
MULT = mybir.AluOpType.mult
AX = mybir.AxisListType.X

P = 128
C = 1024
D = 512
T = 8
HW = 256
NTOK = 1536
G = 3
FLOPS = 2 * (2 * D) * NTOK * C + 2 * (2 * D) * (2 * C) * NTOK
BYTES = 2 * (C * T * HW + C * NTOK + 2 * D * C + 2 * D * NTOK) + 4 * (C * NTOK + 2 * D * 2 * C)


def tile_nlgate_pa_v_kernel(tc, v, a, Wp, bp, Wg, bg, grad_0, grad_1, da, dWp, dWg):
    nc = tc.nc
    with ExitStack() as ctx:
        const = ctx.enter_context(tc.tile_pool(name="const", bufs=1))
        raw = ctx.enter_context(tc.tile_pool(name="raw", bufs=1))
        work = ctx.enter_context(tc.tile_pool(name="work", bufs=1))
        keep = ctx.enter_context(tc.tile_pool(name="keep", bufs=1))
        psum = ctx.enter_context(tc.psum_pool(name="psum", bufs=1))

        identf = const.tile([P, P], F32, name="identf")
        identb = const.tile([P, P], BF16, name="identb")
        make_identity(nc, identf[:])
        make_identity(nc, identb[:])

        v_hbm = v[0].rearrange("(n p i) t h w -> n p i (t h w)", p=P, i=2)
        a_hbm = a[0].rearrange("(n p i) x f -> n p i (x f)", p=P, i=2)
        g0_hbm = grad_0[0].rearrange("(p j) k -> p j k", j=4)
        g1_hbm = grad_1[0].rearrange("(b g r t) w -> g b r (t w)", b=16, g=G, r=8, t=4)
        vt = {}
        at = {}
        wt = {}
        g0 = raw.tile([P, 4, NTOK], BF16, name="g0", align_bytes=64)
        g1 = raw.tile([P, G, 2048], BF16, name="g1", align_bytes=64)

        def raw_tile():
            return raw.tile([P, 4096], BF16, name="r8", tag="r8", bufs=6, align_bytes=64)

        def load_v(n, k):
            if n not in vt:
                vt[n] = raw_tile()[:].rearrange("p (i x) -> p i x", i=2)
            nc.sync.dma_start(out=vt[n][:, k, :], in_=v_hbm[n][:, k, :])

        def load_a(n):
            at[n] = raw_tile()[:, 0 : 2 * NTOK].rearrange("p (i x) -> p i x", i=2)
            nc.sync.dma_start(out=at[n], in_=a_hbm[n])

        def load_w(l):
            wt[l] = raw_tile()[:].rearrange("p (j c) -> p j c", j=4)
            src = (Wp, Wg)[l].rearrange("(p j) c -> p j c", j=4)
            nc.sync.dma_start(out=wt[l], in_=src[:, :, 0:C])

        def load_g0(h):
            nc.sync.dma_start(out=g0[:, h : h + 1, :], in_=g0_hbm[:, h : h + 1, :])

        def load_g1(g, cols=slice(0, 2048)):
            nc.sync.dma_start(out=g1[:, g, cols], in_=g1_hbm[g][:, :, cols])

        def operand(name):
            codes = keep.tile([P, 512], U32, name=name + "c", tag=name + "c", align_bytes=64)
            scales = keep.tile([P, 512], U8, name=name + "s", tag=name + "s", align_bytes=64)
            return codes, scales

        def new_qin():
            return work.tile([P, 2048], BF16, name="qin", tag="qin", bufs=8, align_bytes=64)

        def quantize(name, src, fmt):
            op = operand(name)
            nc.vector.quantize_mx(out=op[0][:].bitcast(fmt), scales=op[1][:], in_=src)
            return op

        def bank():
            return psum.tile([P, 512], F32, name="tp", tag="tp", bufs=4)

        def presort(src, engine):
            s = work.tile([P, 768], F32, name="srt", tag="srt", bufs=5, align_bytes=64)
            i = src.bitcast(F32).rearrange("p (b g r u) -> p u b g r", b=16, g=G, r=8, u=2)
            o = s[:].rearrange("p (g u b r) -> p u b g r", b=16, g=G, r=8, u=2)
            for u in range(2):
                copy(engine, o[:, u], i[:, u])
            return s

        def copy(engine, out, in_):
            if engine == "S":
                nc.scalar.copy(out, in_)
            else:
                nc.vector.tensor_copy(out=out, in_=in_)

        def interleave(engine, src):
            q = new_qin()
            dst = q[:].rearrange("p (c i j) -> p c j i", i=4, j=4)
            copy(engine, dst, src.rearrange("p j (c i) -> p c j i", i=4))
            return q

        def weave(main, fill):
            done = 0
            for i, step in enumerate(main):
                step()
                while done < len(fill) and done < (i + 1) * len(fill) / len(main):
                    fill[done]()
                    done += 1

        g1F = work.tile([P, NTOK * 4], BF16, name="g1F", align_bytes=64)
        g1F_words = g1F[:].bitcast(F32).rearrange("p (b x) -> p b x", b=16)
        dT0 = {}
        dT1 = {}
        dF0 = {}
        dF1 = {}
        wa = {}
        zz = {}
        q1 = {}
        q0 = {}

        banks = {}

        def g1_transpose(g, t0):
            words = g1[:, g, :].bitcast(F32)
            b = bank()
            for k in range(4):
                t, u = t0 + k // 2, k % 2
                nc.tensor.transpose(b[:, k * P : (k + 1) * P], words[:, t * 256 + u : (t + 1) * 256 : 2], identf[:])
            banks["g1", g, t0] = b

        def g1_unload(g, t0, engine):
            b = banks["g1", g, t0]
            dst = g1F_words[:, :, 64 * g : 64 * g + 64].rearrange("p b (r y) -> p b r y", r=8)
            copy(engine, dst[:, :, :, 2 * t0 : 2 * t0 + 4], b[:].rearrange("p (k b r) -> p b r k", k=4, r=8))

        def g1_interleave(g, engine):
            q1[g] = interleave(engine, g1[:, g, :].rearrange("p (t f) -> p t f", t=4))

        def g1_quantize(g):
            dT1[g] = quantize("dT1%d" % g, q1[g][:], E5M2)

        def g1F_quantize(n):
            dF1[n] = quantize("dF1%d" % n, g1F[:, n * 2048 : (n + 1) * 2048], E5M2)

        zsum = {}
        zrep = {}
        zq = {}

        def v_matmul(n, k):
            if ("v", n) not in banks:
                banks["v", n] = bank()
            view = vt[n][:, k, :].rearrange("p (t s w) -> p s t w", t=T, s=8)
            o = banks["v", n][:, k * 256 : (k + 1) * 256].rearrange("p (t w) -> p t w", t=T)
            for s in range(8):
                nc.tensor.matmul(o, identb[:], view[:, s], start=(s == 0), stop=(s == 7))

        def v_reduce(n):
            h, i = n // 2, n % 2
            new_zsum(h)
            b = banks["v", n]
            nc.vector.tensor_reduce(
                out=zsum[h][:, 16 * i : 16 * i + 16], in_=b[:].rearrange("p (x w) -> p x w", w=32), op=ADD, axis=AX
            )

        def new_zsum(h):
            if h not in zsum:
                zsum[h] = work.tile([P, 32], F32, name="zs", tag="zs", bufs=2)

        def v_sum_v(n, k):
            h, i = n // 2, n % 2
            new_zsum(h)
            nc.vector.tensor_reduce(
                out=zsum[h][:, 16 * i + 8 * k : 16 * i + 8 * k + 8],
                in_=vt[n][:, k, :].rearrange("p (t x) -> p t x", t=T),
                op=ADD,
                axis=AX,
            )

        def v_sum_s(n, k, t0):
            h, i = n // 2, n % 2
            new_zsum(h)
            for t in range(t0, t0 + 2):
                junk = work.tile([P, HW], BF16, name="junk", tag="junk", bufs=2)
                c = 16 * i + 8 * k + t
                nc.scalar.activation(
                    out=junk[:],
                    in_=vt[n][:, k, t * HW : (t + 1) * HW],
                    func=mybir.ActivationFunctionType.Copy,
                    accum_out=zsum[h][:, c : c + 1],
                )

        def z_mean(h):
            zrep[h] = work.tile([P, 512], BF16, name="zr", tag="zr", bufs=2)
            nc.vector.tensor_scalar(
                out=zrep[h][:].rearrange("p (x w) -> p x w", w=16),
                in0=zsum[h][:].unsqueeze(2).to_broadcast([P, 32, 16]),
                scalar1=1.0 / HW,
                scalar2=None,
                op0=MULT,
            )

        def z_transpose(h):
            zt = psum.tile([P, 512], BF16, name="tp", tag="tp", bufs=4)
            for i in range(4):
                nc.tensor.transpose(zt[:, i * P : (i + 1) * P], zrep[h][:, i * P : (i + 1) * P], identb[:])
            banks["z", h] = zt

        def z_spread(h, n, engine):
            if h not in zq:
                zq[h] = new_qin()
            dst = zq[h][:, n * 1024 : (n + 1) * 1024].rearrange("q (p i t) -> q p i t", i=2, t=4)
            src = banks["z", h][:, n * 256 : (n + 1) * 256].rearrange("q (i p) -> q p i", i=2)
            copy(engine, dst, src.unsqueeze(3).to_broadcast([P, P, 2, 4]))

        def z_quantize(h):
            zz[h] = [quantize("zz%d" % h, zq[h][:], E4M3)] * G

        dWp_rows = dWp.rearrange("(p j) c -> j p c", j=4)
        dWg_rows = dWg.rearrange("(n p) c -> n p c", p=P)
        da_rows = da[0].rearrange("(n p) i f -> n p (i f)", p=P)

        outs = {}

        def matmuls(pairs, m):
            acc = psum.tile([P, 512], F32, name="acc", tag="acc", bufs=4)
            cols = slice(m * P, (m + 1) * P)
            for k, ((lc, ls), lf, (rc, rs), rf) in enumerate(pairs):
                nc.tensor.matmul_mx(
                    out=acc[:],
                    lhsT=lc[:, cols].bitcast(lf),
                    lhsT_scale=ls[:, cols],
                    rhs=rc[:].bitcast(rf),
                    rhs_scale=rs[:],
                    start=(k == 0),
                    stop=(k == len(pairs) - 1),
                )
            return acc

        def token_unload(l, z, m, h, engine):
            outs[l, z, m, h] = work.tile([P, 512], F32, name="tok", tag="tok", bufs=10)
            copy(engine, outs[l, z, m, h][:], banks[l, z, m, h][:])

        def token_store(l, z, m, h):
            rows = (dWp_rows, dWg_rows)[l]
            c = z * C + h * 512
            nc.sync.dma_start(out=rows[m][:, c : c + 512], in_=outs[l, z, m, h][:])

        def audio_unload(ct, n, engine):
            if ct not in outs:
                outs[ct] = work.tile([P, NTOK], F32, name="aud", tag="aud", bufs=3)
            copy(engine, outs[ct][:, n * 512 : (n + 1) * 512], banks["da", ct, n][:])

        def token_matmul(l, z, m, h):
            dT = (dT0, dT1)[l]
            right = (ac, zz)[z]
            banks[l, z, m, h] = matmuls([(dT[g], E5M2, right[h][g], E4M3) for g in range(G)], m)

        def audio_matmul(ct, n):
            h = ct // 4
            pairs = [(wa[h], E4M3, dF0[n], E5M2), (wa[2 + h], E4M3, dF1[n], E5M2)]
            banks["da", ct, n] = matmuls(pairs, ct % 4)

        def audio_store(ct):
            nc.sync.dma_start(out=da_rows[ct], in_=outs[ct][:])

        s0 = {}

        def g0_presort(j, engine):
            s0[j] = presort(g0[:, j, :], engine)

        def g0_transpose(g, j0):
            b = bank()
            for k in range(4):
                j, u = j0 + k // 2, k % 2
                nc.tensor.transpose(b[:, k * P : (k + 1) * P], s0[j][:, (2 * g + u) * P : (2 * g + u + 1) * P], identf[:])
            banks["g0", g, j0] = b

        def g0_unload(g, j0, engine):
            if g not in q0:
                q0[g] = new_qin()
            copy(
                engine,
                q0[g][:].bitcast(F32)[:, j0 * 256 : j0 * 256 + 512].rearrange("p (j c u) -> p j c u", j=2, u=2),
                banks["g0", g, j0][:].rearrange("p (j u c) -> p j c u", j=2, u=2),
            )

        def g0_quantize(g):
            dT0[g] = quantize("dT0%d" % g, q0[g][:], E5M2)

        qf = {}

        def g0F_interleave(n, engine):
            qf[n] = interleave(engine, g0[:, :, n * 512 : (n + 1) * 512])

        def g0F_quantize(n):
            dF0[n] = quantize("dF0%d" % n, qf[n][:], E5M2)

        qw = {}

        def wa_interleave(l, h, engine):
            qw[l, h] = interleave(engine, wt[l][:, :, h * 512 : (h + 1) * 512])

        def wa_quantize(l, h):
            wa[2 * l + h] = quantize("wa%d" % (2 * l + h), qw[l, h][:], E4M3)

        sa = {}
        qa = {}
        ac = {0: {}, 1: {}}

        def a_presort(n, i, engine):
            sa[n, i] = presort(at[n][:, i, :], engine)

        def a_transpose(n, g):
            b = bank()
            for k in range(4):
                i, u = k // 2, k % 2
                nc.tensor.transpose(b[:, k * P : (k + 1) * P], sa[n, i][:, (2 * g + u) * P : (2 * g + u + 1) * P], identf[:])
            banks["a", n, g] = b

        def a_unload(n, g, engine):
            h = n // 2
            if (h, g) not in qa:
                qa[h, g] = new_qin()
            words = qa[h, g][:].bitcast(F32)[:, (n % 2) * 512 : (n % 2) * 512 + 512]
            copy(engine, words.rearrange("q (c k) -> q c k", k=4), banks["a", n, g][:].rearrange("q (k c) -> q c k", k=4))

        def a_quantize(h, g):
            ac[h][g] = quantize("a%d%d" % (h, g), qa[h, g][:], E4M3)

        with tc.manual_schedule():
            load_g1(0, slice(0, 1024))
            load_g1(0, slice(1024, 2048))
            load_g1(1)
            load_g1(2)
            load_v(0, 0)
            load_v(0, 1)
            load_v(1, 0)
            load_v(1, 1)
            load_g0(0)
            load_g0(1)
            load_g0(2)
            load_g0(3)
            load_v(2, 0)
            load_v(2, 1)
            load_v(3, 0)
            load_v(3, 1)
            load_w(0)
            load_w(1)
            load_a(0)
            load_a(1)
            load_a(2)
            load_a(3)
            g1_transpose(0, 0)
            g1_interleave(0, "V")
            g1_transpose(0, 2)
            g1_unload(0, 0, "S")
            g1_interleave(1, "S")
            g1_transpose(1, 2)
            g1_unload(0, 2, "V")
            g1_transpose(1, 0)
            g1_quantize(0)
            g1_transpose(2, 2)
            g1_unload(1, 2, "V")
            g1_transpose(2, 0)
            g1_unload(1, 0, "V")
            v_matmul(0, 0)
            g1_unload(2, 2, "V")
            g1_interleave(2, "S")
            g1_quantize(1)
            v_matmul(0, 1)
            g1_unload(2, 0, "V")
            g1F_quantize(2)
            v_matmul(1, 0)
            g1F_quantize(0)
            g1_quantize(2)
            v_matmul(1, 1)
            v_reduce(0)
            g0_presort(0, "S")
            g1F_quantize(1)
            g0_presort(1, "V")
            v_reduce(1)
            g0_transpose(0, 0)
            g0_transpose(1, 0)
            g0_presort(2, "V")
            g0_unload(0, 0, "S")
            g0_transpose(2, 0)
            z_mean(0)
            g0_unload(1, 0, "S")
            g0_presort(3, "V")
            z_transpose(0)
            g0F_interleave(1, "V")
            g0_unload(2, 0, "S")
            g0_transpose(2, 2)
            g0_transpose(0, 2)
            z_spread(0, 0, "S")
            v_matmul(2, 0)
            z_spread(0, 1, "V")
            g0_unload(0, 2, "S")
            v_matmul(2, 1)
            g0F_interleave(2, "S")
            g0_unload(2, 2, "V")
            z_quantize(0)
            g0_transpose(1, 2)
            g0_quantize(2)
            token_matmul(1, 1, 1, 0)
            v_reduce(2)
            g0_unload(1, 2, "S")
            g0_quantize(0)
            token_matmul(1, 1, 3, 0)
            v_sum_s(3, 0, 0)
            g0F_quantize(2)
            token_matmul(1, 1, 2, 0)
            token_unload(1, 1, 1, 0, "S")
            g0_quantize(1)
            wa_interleave(0, 0, "S")
            token_unload(1, 1, 3, 0, "V")
            token_store(1, 1, 1, 0)
            token_matmul(0, 1, 1, 0)
            token_unload(1, 1, 2, 0, "V")
            token_store(1, 1, 3, 0)
            token_matmul(0, 1, 3, 0)
            g0F_quantize(1)
            token_store(1, 1, 2, 0)
            token_unload(0, 1, 1, 0, "V")
            token_matmul(0, 1, 0, 0)
            wa_interleave(1, 0, "V")
            token_unload(0, 1, 3, 0, "S")
            token_store(0, 1, 1, 0)
            v_sum_s(3, 1, 0)
            token_matmul(0, 1, 2, 0)
            token_store(0, 1, 3, 0)
            a_presort(0, 0, "S")
            a_presort(0, 1, "V")
            token_matmul(1, 1, 0, 0)
            token_unload(0, 1, 0, 0, "V")
            token_unload(0, 1, 2, 0, "S")
            wa_quantize(0, 0)
            token_store(0, 1, 0, 0)
            a_transpose(0, 0)
            v_sum_s(3, 0, 2)
            wa_quantize(1, 0)
            token_store(0, 1, 2, 0)
            a_transpose(0, 2)
            a_unload(0, 0, "S")
            a_transpose(0, 1)
            token_unload(1, 1, 0, 0, "V")
            audio_matmul(2, 2)
            a_unload(0, 2, "S")
            a_presort(1, 0, "V")
            a_unload(0, 1, "S")
            audio_matmul(3, 1)
            g0F_interleave(0, "V")
            token_store(1, 1, 0, 0)
            a_presort(1, 1, "S")
            audio_matmul(1, 1)
            audio_matmul(3, 2)
            v_sum_s(3, 0, 6)
            audio_unload(3, 1, "V")
            a_transpose(1, 1)
            a_presort(3, 0, "S")
            a_presort(3, 1, "V")
            a_transpose(1, 2)
            audio_unload(2, 2, "V")
            a_transpose(1, 0)
            audio_unload(1, 1, "S")
            a_transpose(3, 0)
            g0F_quantize(0)
            a_unload(1, 0, "S")
            audio_matmul(2, 1)
            a_unload(3, 0, "V")
            a_presort(2, 0, "S")
            audio_matmul(3, 0)
            audio_unload(3, 2, "V")
            audio_matmul(1, 0)
            audio_unload(2, 1, "V")
            a_unload(1, 2, "S")
            audio_unload(3, 0, "V")
            v_sum_s(3, 1, 4)
            audio_matmul(2, 0)
            a_quantize(0, 2)
            a_presort(2, 1, "S")
            audio_matmul(1, 2)
            audio_store(3)
            a_unload(1, 1, "V")
            audio_matmul(0, 2)
            audio_unload(2, 0, "S")
            audio_unload(1, 2, "V")
            a_transpose(2, 2)
            v_sum_s(3, 1, 6)
            audio_store(2)
            a_quantize(0, 1)
            a_transpose(2, 0)
            a_unload(2, 2, "S")
            a_transpose(2, 1)
            audio_unload(1, 0, "V")
            a_transpose(3, 1)
            wa_interleave(1, 1, "S")
            a_transpose(3, 2)
            a_unload(2, 1, "V")
            audio_store(1)
            audio_matmul(0, 0)
            a_quantize(0, 0)
            audio_matmul(0, 1)
            audio_unload(0, 2, "V")
            token_matmul(0, 0, 0, 0)
            audio_unload(0, 0, "V")
            a_unload(3, 2, "S")
            audio_unload(0, 1, "V")
            token_matmul(0, 0, 1, 0)
            a_unload(3, 1, "S")
            wa_quantize(1, 1)
            audio_store(0)
            token_unload(0, 0, 0, 0, "S")
            a_quantize(1, 2)
            token_matmul(0, 0, 2, 0)
            token_unload(0, 0, 1, 0, "S")
            a_quantize(1, 1)
            token_store(0, 0, 0, 0)
            wa_interleave(0, 1, "S")
            token_matmul(1, 0, 2, 0)
            token_store(0, 0, 1, 0)
            a_unload(2, 0, "V")
            token_unload(0, 0, 2, 0, "V")
            token_matmul(1, 0, 0, 0)
            a_quantize(1, 0)
            token_store(0, 0, 2, 0)
            token_matmul(1, 0, 1, 0)
            token_unload(1, 0, 0, 0, "V")
            token_unload(1, 0, 2, 0, "S")
            wa_quantize(0, 1)
            token_matmul(1, 0, 2, 1)
            token_store(1, 0, 0, 0)
            token_unload(1, 0, 1, 0, "S")
            token_store(1, 0, 2, 0)
            v_sum_s(3, 0, 4)
            audio_matmul(6, 2)
            token_store(1, 0, 1, 0)
            token_unload(1, 0, 2, 1, "V")
            v_sum_s(3, 1, 2)
            audio_matmul(7, 1)
            audio_unload(6, 2, "V")
            token_store(1, 0, 2, 1)
            audio_matmul(7, 2)
            z_mean(1)
            audio_unload(7, 1, "V")
            audio_matmul(6, 0)
            audio_unload(7, 2, "V")
            audio_matmul(6, 1)
            audio_unload(6, 0, "S")
            token_matmul(1, 0, 1, 1)
            audio_unload(6, 1, "S")
            audio_matmul(4, 1)
            audio_store(6)
            token_unload(1, 0, 1, 1, "S")
            token_matmul(1, 0, 0, 1)
            audio_unload(4, 1, "S")
            token_store(1, 0, 1, 1)
            audio_matmul(4, 0)
            token_unload(1, 0, 0, 1, "V")
            audio_matmul(4, 2)
            audio_unload(4, 0, "S")
            token_store(1, 0, 0, 1)
            audio_matmul(5, 2)
            audio_unload(4, 2, "V")
            token_matmul(0, 0, 2, 1)
            audio_store(4)
            audio_unload(5, 2, "S")
            token_matmul(0, 0, 3, 0)
            token_unload(0, 0, 2, 1, "S")
            token_matmul(1, 0, 3, 1)
            token_store(0, 0, 2, 1)
            token_unload(0, 0, 3, 0, "V")
            token_matmul(0, 0, 1, 1)
            token_store(0, 0, 3, 0)
            token_unload(1, 0, 3, 1, "V")
            audio_matmul(5, 1)
            token_store(1, 0, 3, 1)
            token_unload(0, 0, 1, 1, "S")
            z_transpose(1)
            audio_unload(5, 1, "S")
            token_store(0, 0, 1, 1)
            token_matmul(0, 0, 0, 1)
            z_spread(1, 0, "V")
            token_matmul(0, 0, 3, 1)
            token_unload(0, 0, 0, 1, "S")
            z_spread(1, 1, "V")
            token_matmul(1, 0, 3, 0)
            token_store(0, 0, 0, 1)
            token_unload(0, 0, 3, 1, "V")
            audio_matmul(5, 0)
            z_quantize(1)
            token_store(0, 0, 3, 1)
            token_unload(1, 0, 3, 0, "S")
            audio_matmul(7, 0)
            audio_unload(5, 0, "V")
            token_store(1, 0, 3, 0)
            token_matmul(1, 1, 0, 1)
            audio_unload(7, 0, "V")
            audio_store(5)
            token_matmul(0, 1, 1, 1)
            audio_store(7)
            token_unload(1, 1, 0, 1, "S")
            token_matmul(0, 1, 3, 1)
            token_store(1, 1, 0, 1)
            token_unload(0, 1, 1, 1, "S")
            token_matmul(1, 1, 2, 1)
            token_store(0, 1, 1, 1)
            token_unload(0, 1, 3, 1, "V")
            token_matmul(0, 1, 0, 1)
            token_store(0, 1, 3, 1)
            token_unload(1, 1, 2, 1, "S")
            token_matmul(1, 1, 3, 1)
            token_store(1, 1, 2, 1)
            token_unload(0, 1, 0, 1, "S")
            token_matmul(0, 1, 2, 1)
            token_store(0, 1, 0, 1)
            token_unload(1, 1, 3, 1, "S")
            token_matmul(1, 1, 1, 1)
            token_store(1, 1, 3, 1)
            token_unload(0, 1, 2, 1, "S")
            token_store(0, 1, 2, 1)
            token_unload(1, 1, 1, 1, "S")
            token_store(1, 1, 1, 1)
